import numpy as np
import ml_dtypes


def mxq(x, axis, fmt="e4m3"):
    dtype, down = {"e4m3": (ml_dtypes.float8_e4m3fn, 7), "e5m2": (ml_dtypes.float8_e5m2, 14)}[fmt]
    v = np.moveaxis(np.asarray(x, np.float32).astype(ml_dtypes.bfloat16).astype(np.float64), axis, -1)
    blocks = v.reshape(v.shape[:-1] + (-1, 32))
    amax = np.abs(blocks).max(-1, keepdims=True)
    byte = np.maximum(np.where(amax > 0, np.frexp(amax)[1] - 1 + 127, 0) - down, 1)
    scale = np.exp2(byte - 127.0)
    codes = (blocks / scale).astype(np.float32).astype(dtype).astype(np.float64)
    return np.moveaxis((codes * scale).reshape(v.shape), -1, axis)


WIDE = False


def mx_kscale(k):
    if not WIDE:
        return np.ones(k)
    levels = np.array([10, -10, 5, -5, 0])
    a = np.random.permutation(np.resize(levels, k // 512 * 4)).reshape(k // 512, 4)
    idx = np.arange(k)
    return np.exp2(a[idx // 512, idx % 128 // 32])


BF16 = ml_dtypes.bfloat16


def bf(x):
    return np.asarray(x, np.float32).astype(BF16)


def f64(x):
    return np.asarray(x).astype(np.float64)


E, B, IN, H, O = 5, 896, 71, 1024, 64
O2 = O + O


def silu(v):
    return v / (1.0 + np.exp(-v))


def softplus(v):
    return np.maximum(v, 0.0) + np.log(1.0 + np.exp(-np.abs(v)))


def setup_inputs():
    s = mx_kscale(H)
    return {"h2": bf(silu(np.random.standard_normal((E, B, H))) * s),
            "w3": bf(np.random.standard_normal((E, H, H)) * 1.6 / np.sqrt(H) / s[:, None]),
            "b3": bf(np.random.standard_normal((E, 1, H)) * 0.2),
            "w4": bf(np.random.standard_normal((E, H, O2)) * 2.5 / np.sqrt(H)),
            "b4": bf(np.random.standard_normal((E, 1, O2)) * 0.2),
            "max_logvar": bf(0.5 + 0.1 * np.random.standard_normal((1, O))),
            "min_logvar": bf(-1.5 + 0.1 * np.random.standard_normal((1, O)))}


def reference(h2, w3, b3, w4, b4, max_logvar, min_logvar):
    h3 = silu((mxq(f64(h2), 2, "e4m3") @ mxq(f64(w3), 1, "e4m3")) + f64(b3))
    o = (mxq(h3, 2, "e4m3") @ mxq(f64(w4), 1, "e4m3")) + f64(b4)
    mean, logvar = o[..., :O], o[..., O:]
    logvar = f64(max_logvar) - softplus(f64(max_logvar) - logvar)
    logvar = f64(min_logvar) + softplus(logvar - f64(min_logvar))
    return mean, logvar

@@ -1,0 +1,339 @@
+import concourse.mybir as mybir
+from concourse.masks import make_identity
+
+F32 = mybir.dt.float32
+BF16 = mybir.dt.bfloat16
+U32 = mybir.dt.uint32
+U8 = mybir.dt.uint8
+FP8X4 = mybir.dt.float8_e4m3fn_x4
+ACT = mybir.ActivationFunctionType
+ALU = mybir.AluOpType
+
+P = 128
+PACK = 4
+K_PASS = P * PACK
+E, B, H, O = 5, 896, 1024, 64
+O2 = 2 * O
+PASSES = H // K_PASS
+ROW_TILES = B // P
+W3_CHUNK = 512
+COLUMN_CHUNKS = ((0, 512), (512, 768), (768, 896))
+ROW_TILES_PER_BANK = 4
+
+FLOPS = 2 * E * B * H * (H + O2)
+
+
+def tile_ensembledynamicsmodel_pa_t_kernel(
+    tc, h2, w3, b3, w4, b4, max_logvar, min_logvar, out_0, out_1
+):
+    nc = tc.nc
+
+    def interleave(copy, grouped, planes):
+        copy(
+            out=grouped.rearrange("p (c i) t -> p c t i", i=4),
+            in_=planes.rearrange("p t (c i) -> p c t i", i=4),
+        )
+
+    with tc.manual_schedule(), tc.tile_pool(name="consts", bufs=1) as consts, tc.tile_pool(
+        name="loads", bufs=2
+    ) as loads, tc.tile_pool(name="work", bufs=2) as work, tc.tile_pool(
+        name="codes", bufs=2
+    ) as codes, tc.psum_pool(name="psum", bufs=2) as psum:
+        ident_words = consts.tile([P, P], F32)
+        make_identity(nc, ident_words[:])
+        ident_bf16 = consts.tile([P, P], BF16)
+        make_identity(nc, ident_bf16[:])
+        half = consts.tile([P, 1], F32)
+        nc.vector.memset(half[:], 0.5)
+        b3_rows = consts.tile([P, P], BF16)
+        nc.vector.memset(b3_rows[:], 0.0)
+
+        w3_rows, h2_rows, w4_rows = {}, {}, {}
+        w3_codes, w3_scales, h2_grouped, h2_codes, h2_scales = {}, {}, {}, {}, {}
+        h3_planes, h3_codes, h3_scales, w4_codes, w4_scales = {}, {}, {}, {}, {}
+
+        def load(e):
+            w3_rows[e] = loads.tile([P, PASSES, PACK, H], BF16, name="w3_rows")
+            for g in range(PASSES):
+                nc.sync.dma_start(
+                    out=w3_rows[e][:, g].rearrange("p (u i) n -> p u (i n)", i=2),
+                    in_=w3[e, g * K_PASS : (g + 1) * K_PASS, :].rearrange(
+                        "(u p i) n -> p u (i n)", u=2, i=2
+                    ),
+                )
+            h2_rows[e] = loads.tile([P, ROW_TILES * H], BF16, name="h2_rows")
+            nc.sync.dma_start(
+                out=h2_rows[e][:], in_=h2[e].rearrange("(p r) k -> p (r k)", r=ROW_TILES)
+            )
+            w4_rows[e] = loads.tile([P, PASSES * PACK, O2], BF16, name="w4_rows")
+            nc.sync.dma_start(out=w4_rows[e][:], in_=w4[e].rearrange("(j p) o -> p j o", p=P))
+
+        def quantise_w3(e):
+            w3_codes[e] = codes.tile([P, PASSES, H], U32, name="w3_codes", align_bytes=64)
+            w3_scales[e] = codes.tile([P, PASSES, H], U8, name="w3_scales", align_bytes=64)
+            chunks = [(g, n0) for g in range(PASSES) for n0 in range(0, H, W3_CHUNK)]
+            grouped = []
+            for index, (g, n0) in enumerate(chunks):
+                w3_grouped = work.tile(
+                    [P, W3_CHUNK, PACK], BF16, name="w3_grouped", bufs=len(chunks), align_bytes=64
+                )
+                grouped.append(w3_grouped)
+                copy = nc.scalar.copy if index == 0 else nc.vector.tensor_copy
+                interleave(copy, w3_grouped[:], w3_rows[e][:, g, :, n0 : n0 + W3_CHUNK])
+            for (g, n0), w3_grouped in zip(chunks, grouped):
+                nc.vector.quantize_mx(
+                    out=w3_codes[e][:, g, n0 : n0 + W3_CHUNK].bitcast(FP8X4),
+                    scales=w3_scales[e][:, g, n0 : n0 + W3_CHUNK],
+                    in_=w3_grouped[:].rearrange("p n t -> p (n t)"),
+                )
+
+        def regroup_w4(e):
+            w4_grouped = work.tile([P, PASSES, O2, PACK], BF16, name="w4_grouped", align_bytes=64)
+            nc.vector.tensor_copy(
+                out=w4_grouped[:], in_=w4_rows[e][:].rearrange("p (g t) o -> p g o t", t=PACK)
+            )
+            return w4_grouped
+
+        def quantise_w4(e, w4_grouped):
+            w4_codes[e] = codes.tile([P, PASSES, O2], U32, name="w4_codes", align_bytes=64)
+            w4_scales[e] = codes.tile([P, PASSES, O2], U8, name="w4_scales", align_bytes=64)
+            nc.vector.quantize_mx(
+                out=w4_codes[e][:].rearrange("p g o -> p (g o)").bitcast(FP8X4),
+                scales=w4_scales[e][:].rearrange("p g o -> p (g o)"),
+                in_=w4_grouped[:].rearrange("p g o t -> p (g o t)"),
+            )
+
+        def transpose_h2(e):
+            h2_grouped[e] = work.tile(
+                [P, PASSES * B * PACK], BF16, name="h2_grouped", bufs=1, align_bytes=64
+            )
+            words_in = h2_rows[e][:].bitcast(F32)
+            words_out = h2_grouped[e][:].bitcast(F32).rearrange(
+                "p (g c u) -> p g c u", g=PASSES, u=2
+            )
+            blocks = H // 2 // P
+            for r in range(ROW_TILES):
+                flipped = psum.tile([P, blocks, P], F32, name="flipped")
+                for j in range(blocks):
+                    w0 = (r * blocks + j) * P
+                    nc.tensor.transpose(flipped[:, j, :], words_in[:, w0 : w0 + P], ident_words[:])
+                nc.scalar.copy(
+                    out=words_out[:, :, r * P : (r + 1) * P, :],
+                    in_=flipped[:].rearrange("p (g u) c -> p g c u", u=2),
+                )
+
+        def quantise_h2(e):
+            h2_codes[e] = codes.tile([P, PASSES, B], U32, name="h2_codes", align_bytes=64)
+            h2_scales[e] = codes.tile([P, PASSES, B], U8, name="h2_scales", align_bytes=64)
+            for c0, c1 in COLUMN_CHUNKS:
+                for g in range(PASSES):
+                    nc.vector.quantize_mx(
+                        out=h2_codes[e][:, g, c0:c1].bitcast(FP8X4),
+                        scales=h2_scales[e][:, g, c0:c1],
+                        in_=h2_grouped[e][:, (g * B + c0) * PACK : (g * B + c1) * PACK],
+                    )
+
+        def layer1(e, g_out):
+            h3_planes[e, g_out] = work.tile([P, PACK, B], BF16, name="h3_planes")
+            for t in range(PACK):
+                m = g_out * PACK + t
+                acc_wide = psum.tile([P, 512], F32, name="acc_wide")
+                acc_rest = psum.tile([P, 384], F32, name="acc_rest")
+                targets = (acc_wide[:, 0:512], acc_rest[:, 0:256], acc_rest[:, 256:384])
+                for (c0, c1), target in zip(COLUMN_CHUNKS, targets):
+                    for g in range(PASSES):
+                        nc.tensor.matmul_mx(
+                            out=target,
+                            lhsT=w3_codes[e][:, g, m * P : (m + 1) * P].bitcast(FP8X4),
+                            lhsT_scale=w3_scales[e][:, g, m * P : (m + 1) * P],
+                            rhs=h2_codes[e][:, g, c0:c1].bitcast(FP8X4),
+                            rhs_scale=h2_scales[e][:, g, c0:c1],
+                            start=(g == 0),
+                            stop=(g == PASSES - 1),
+                        )
+                bias = b3_columns[:, e * (H // P) + m : e * (H // P) + m + 1]
+                nc.scalar.activation(
+                    out=h3_planes[e, g_out][:, t, 0:512], in_=acc_wide[:], func=ACT.Silu, bias=bias
+                )
+                nc.scalar.activation(
+                    out=h3_planes[e, g_out][:, t, 512:B], in_=acc_rest[:], func=ACT.Silu, bias=bias
+                )
+
+        def quantise_h3(e, g_out):
+            if g_out == 0:
+                h3_codes[e] = codes.tile([P, PASSES, B], U32, name="h3_codes", align_bytes=64)
+                h3_scales[e] = codes.tile([P, PASSES, B], U8, name="h3_scales", align_bytes=64)
+            h3_grouped = work.tile([P, B, PACK], BF16, name="h3_grouped", align_bytes=64)
+            for c0, c1 in COLUMN_CHUNKS:
+                interleave(
+                    nc.vector.tensor_copy, h3_grouped[:, c0:c1, :], h3_planes[e, g_out][:, :, c0:c1]
+                )
+            for c0, c1 in COLUMN_CHUNKS:
+                nc.vector.quantize_mx(
+                    out=h3_codes[e][:, g_out, c0:c1].bitcast(FP8X4),
+                    scales=h3_scales[e][:, g_out, c0:c1],
+                    in_=h3_grouped[:, c0:c1, :].rearrange("p c t -> p (c t)"),
+                )
+
+        def layer2(e):
+            offset = work.tile([P, O], F32, name="offset")
+            nc.vector.tensor_tensor(
+                out=offset[:], in0=max_rows[:], in1=b4_rows[:, e, O:O2], op=ALU.subtract
+            )
+            mean = work.tile([P, ROW_TILES, O], F32, name="mean")
+            for r0 in range(0, ROW_TILES, ROW_TILES_PER_BANK):
+                count = min(ROW_TILES_PER_BANK, ROW_TILES - r0)
+                acc_out = psum.tile([P, ROW_TILES_PER_BANK, O2], F32, name="acc_out")
+                for r in range(r0, r0 + count):
+                    for g in range(PASSES):
+                        nc.tensor.matmul_mx(
+                            out=acc_out[:, r - r0, :],
+                            lhsT=h3_codes[e][:, g, r * P : (r + 1) * P].bitcast(FP8X4),
+                            lhsT_scale=h3_scales[e][:, g, r * P : (r + 1) * P],
+                            rhs=w4_codes[e][:, g, :].bitcast(FP8X4),
+                            rhs_scale=w4_scales[e][:, g, :],
+                            start=(g == 0),
+                            stop=(g == PASSES - 1),
+                        )
+                nc.vector.tensor_tensor(
+                    out=mean[:, r0 : r0 + count, :],
+                    in0=acc_out[:, 0:count, 0:O],
+                    in1=b4_rows[:, e, 0:O].unsqueeze(1).to_broadcast([P, count, O]),
+                    op=ALU.add,
+                )
+                nc.vector.tensor_tensor(
+                    out=above[:, e, r0 : r0 + count, :],
+                    in0=offset[:].unsqueeze(1).to_broadcast([P, count, O]),
+                    in1=acc_out[:, 0:count, O2 - O : O2],
+                    op=ALU.subtract,
+                )
+            nc.sync.dma_start(
+                out=out_0[e].rearrange("(p r) o -> p r o", r=ROW_TILES), in_=mean[:]
+            )
+
+        def flat(tile_of_members, e):
+            return tile_of_members[:, e].rearrange("p r o -> p (r o)")
+
+        def over_rows(row):
+            return row.unsqueeze(1).to_broadcast([P, ROW_TILES, O])
+
+        def magnitude_on_scalar(members):
+            for e in members:
+                nc.scalar.activation(out=flat(soft, e), in_=flat(above, e), func=ACT.Abs)
+
+        def tanh_of_half(members):
+            for e in members:
+                nc.scalar.activation(out=flat(soft, e), in_=flat(soft, e), func=ACT.Tanh, scale=0.5)
+
+        def log_sigmoid(members):
+            for e in members:
+                nc.scalar.activation(
+                    out=flat(soft, e), in_=flat(soft, e), func=ACT.Ln, scale=0.5, bias=half[:]
+                )
+
+        def hard_part_of_first_bound(members):
+            for e in members:
+                nc.vector.scalar_tensor_tensor(
+                    out=hard[:, e],
+                    in0=above[:, e],
+                    scalar=0.0,
+                    in1=over_rows(span[:]),
+                    op0=ALU.max,
+                    op1=ALU.subtract,
+                )
+
+        load(0)
+        nc.sync.dma_start(
+            out=b3_rows[0 : E * (H // P), :], in_=b3.rearrange("e a (m p) -> (e a m) p", p=P)
+        )
+        load(1)
+        b4_rows = consts.tile([P, E, O2], BF16)
+        nc.sync.dma_start(
+            out=b4_rows[:].rearrange("p e o -> p (e o)"),
+            in_=b4.rearrange("e a o -> (e a o)").partition_broadcast(P),
+        )
+        max_rows = consts.tile([P, O], BF16)
+        nc.sync.dma_start(
+            out=max_rows[:], in_=max_logvar.rearrange("a o -> (a o)").partition_broadcast(P)
+        )
+        min_rows = consts.tile([P, O], BF16)
+        nc.sync.dma_start(
+            out=min_rows[:], in_=min_logvar.rearrange("a o -> (a o)").partition_broadcast(P)
+        )
+
+        above = consts.tile([P, E, ROW_TILES, O], F32)
+        hard = consts.tile([P, E, ROW_TILES, O], F32)
+        soft = consts.tile([P, E, ROW_TILES, O], F32)
+        span = consts.tile([P, O], F32)
+
+        quantise_w3(0)
+        transpose_h2(0)
+        w4_grouped = regroup_w4(0)
+        quantise_h2(0)
+        quantise_w4(0, w4_grouped)
+        b3_flipped = psum.tile([P, P], BF16, name="b3_flipped", tag="flipped")
+        nc.tensor.transpose(b3_flipped[:], b3_rows[:], ident_bf16[:])
+        b3_columns = consts.tile([P, E * (H // P)], F32)
+        nc.vector.tensor_copy(out=b3_columns[:], in_=b3_flipped[:, 0 : E * (H // P)])
+
+        for e in range(E):
+            if e + 2 < E:
+                load(e + 2)
+            if e + 1 < E:
+                quantise_w3(e + 1)
+            layer1(e, 0)
+            if e + 1 < E:
+                w4_grouped = regroup_w4(e + 1)
+            quantise_h3(e, 0)
+            if e + 1 < E:
+                quantise_w4(e + 1, w4_grouped)
+            layer1(e, 1)
+            if e + 1 < E:
+                transpose_h2(e + 1)
+            else:
+                nc.vector.tensor_tensor(
+                    out=span[:], in0=max_rows[:], in1=min_rows[:], op=ALU.subtract
+                )
+                magnitude_on_scalar(range(E - 1))
+                tanh_of_half(range(E - 1))
+                hard_part_of_first_bound(range(E - 1))
+            quantise_h3(e, 1)
+            if e + 1 < E:
+                quantise_h2(e + 1)
+            layer2(e)
+
+        magnitude_on_scalar([E - 1])
+        tanh_of_half([E - 1])
+        hard_part_of_first_bound([E - 1])
+        log_sigmoid(range(E))
+        for e in range(E):
+            nc.vector.tensor_tensor(
+                out=above[:, e], in0=soft[:, e], in1=hard[:, e], op=ALU.subtract
+            )
+        for e in range(E):
+            nc.vector.scalar_tensor_tensor(
+                out=soft[:, e],
+                in0=above[:, e],
+                scalar=-1.0,
+                in1=above[:, e],
+                op0=ALU.mult,
+                op1=ALU.max,
+            )
+        for e in range(E):
+            nc.vector.scalar_tensor_tensor(
+                out=hard[:, e],
+                in0=above[:, e],
+                scalar=0.0,
+                in1=over_rows(min_rows[:]),
+                op0=ALU.max,
+                op1=ALU.add,
+            )
+        tanh_of_half(range(E))
+        log_sigmoid(range(E))
+        for e in range(E):
+            nc.vector.tensor_tensor(
+                out=above[:, e], in0=hard[:, e], in1=soft[:, e], op=ALU.subtract
+            )
+            nc.sync.dma_start(
+                out=out_1[e].rearrange("(p r) o -> p r o", r=ROW_TILES), in_=above[:, e]
+            )

@@ -16,9 +16,10 @@ E, B, H, O = 5, 896, 1024, 64
 O2 = 2 * O
 PASSES = H // K_PASS
 ROW_TILES = B // P
+FEATURE_TILES = H // P
 W3_CHUNK = 512
-COLUMN_CHUNKS = ((0, 512), (512, 768), (768, 896))
-ROW_TILES_PER_BANK = 4
+COLUMN_HALVES = (((0, 512),), ((512, 768), (768, 896)))
+BANK_COLUMNS = 512
 
 FLOPS = 2 * E * B * H * (H + O2)
 
@@ -27,6 +28,10 @@ def tile_ensembledynamicsmodel_pa_t_kernel(
     tc, h2, w3, b3, w4, b4, max_logvar, min_logvar, out_0, out_1
 ):
     nc = tc.nc
+
+    def bounds_of(half):
+        chunks = COLUMN_HALVES[half]
+        return chunks[0][0], chunks[-1][1]
 
     def interleave(copy, grouped, planes):
         copy(
@@ -39,21 +44,25 @@ def tile_ensembledynamicsmodel_pa_t_kernel(
     ) as loads, tc.tile_pool(name="work", bufs=2) as work, tc.tile_pool(
         name="codes", bufs=2
     ) as codes, tc.psum_pool(name="psum", bufs=2) as psum:
-        ident_words = consts.tile([P, P], F32)
-        make_identity(nc, ident_words[:])
-        ident_bf16 = consts.tile([P, P], BF16)
-        make_identity(nc, ident_bf16[:])
-        half = consts.tile([P, 1], F32)
-        nc.vector.memset(half[:], 0.5)
-        b3_rows = consts.tile([P, P], BF16)
-        nc.vector.memset(b3_rows[:], 0.0)
-
-        w3_rows, h2_rows, w4_rows = {}, {}, {}
+        w3_rows, h2_rows, w4_rows, w4_grouped = {}, {}, {}, {}
         w3_codes, w3_scales, h2_grouped, h2_codes, h2_scales = {}, {}, {}, {}, {}
-        h3_planes, h3_codes, h3_scales, w4_codes, w4_scales = {}, {}, {}, {}, {}
+        h3_planes, h3_grouped, h3_codes, h3_scales, w4_codes, w4_scales = {}, {}, {}, {}, {}, {}
+        acc_out, mean, above, offset, tanh_above, tanh_w = {}, {}, {}, {}, {}, {}
 
         def load(e):
+            if e >= E:
+                return
+            h2_rows[e] = loads.tile([P, ROW_TILES, H], BF16, name="h2_rows")
             w3_rows[e] = loads.tile([P, PASSES, PACK, H], BF16, name="w3_rows")
+            w4_rows[e] = loads.tile([P, PASSES * PACK, O2], BF16, name="w4_rows")
+
+            def load_h2(half):
+                lo, hi = bounds_of(half)
+                nc.sync.dma_start(
+                    out=h2_rows[e][:, lo // P : hi // P, :],
+                    in_=h2[e].rearrange("(p r) k -> p r k", r=ROW_TILES)[:, lo // P : hi // P, :],
+                )
+
             for g in range(PASSES):
                 nc.sync.dma_start(
                     out=w3_rows[e][:, g].rearrange("p (u i) n -> p u (i n)", i=2),
@@ -61,58 +70,66 @@ def tile_ensembledynamicsmodel_pa_t_kernel(
                         "(u p i) n -> p u (i n)", u=2, i=2
                     ),
                 )
-            h2_rows[e] = loads.tile([P, ROW_TILES * H], BF16, name="h2_rows")
-            nc.sync.dma_start(
-                out=h2_rows[e][:], in_=h2[e].rearrange("(p r) k -> p (r k)", r=ROW_TILES)
-            )
-            w4_rows[e] = loads.tile([P, PASSES * PACK, O2], BF16, name="w4_rows")
+            load_h2(0)
+            load_h2(1)
             nc.sync.dma_start(out=w4_rows[e][:], in_=w4[e].rearrange("(j p) o -> p j o", p=P))
 
         def quantise_w3(e):
+            if e >= E:
+                return
             w3_codes[e] = codes.tile([P, PASSES, H], U32, name="w3_codes", align_bytes=64)
             w3_scales[e] = codes.tile([P, PASSES, H], U8, name="w3_scales", align_bytes=64)
-            chunks = [(g, n0) for g in range(PASSES) for n0 in range(0, H, W3_CHUNK)]
-            grouped = []
-            for index, (g, n0) in enumerate(chunks):
-                w3_grouped = work.tile(
-                    [P, W3_CHUNK, PACK], BF16, name="w3_grouped", bufs=len(chunks), align_bytes=64
-                )
-                grouped.append(w3_grouped)
-                copy = nc.scalar.copy if index == 0 else nc.vector.tensor_copy
-                interleave(copy, w3_grouped[:], w3_rows[e][:, g, :, n0 : n0 + W3_CHUNK])
-            for (g, n0), w3_grouped in zip(chunks, grouped):
-                nc.vector.quantize_mx(
-                    out=w3_codes[e][:, g, n0 : n0 + W3_CHUNK].bitcast(FP8X4),
-                    scales=w3_scales[e][:, g, n0 : n0 + W3_CHUNK],
-                    in_=w3_grouped[:].rearrange("p n t -> p (n t)"),
-                )
+            for n0 in range(0, H, W3_CHUNK):
+                grouped = []
+                for g in range(PASSES):
+                    w3_grouped = work.tile(
+                        [P, W3_CHUNK, PACK], BF16, name="w3_grouped", bufs=4, align_bytes=64
+                    )
+                    grouped.append(w3_grouped)
+                    copy = nc.scalar.copy if (n0 > 0 and g == 0) else nc.vector.tensor_copy
+                    interleave(copy, w3_grouped[:], w3_rows[e][:, g, :, n0 : n0 + W3_CHUNK])
+                for g in range(PASSES):
+                    nc.vector.quantize_mx(
+                        out=w3_codes[e][:, g, n0 : n0 + W3_CHUNK].bitcast(FP8X4),
+                        scales=w3_scales[e][:, g, n0 : n0 + W3_CHUNK],
+                        in_=grouped[g][:].rearrange("p n t -> p (n t)"),
+                    )
 
         def regroup_w4(e):
-            w4_grouped = work.tile([P, PASSES, O2, PACK], BF16, name="w4_grouped", align_bytes=64)
-            nc.vector.tensor_copy(
-                out=w4_grouped[:], in_=w4_rows[e][:].rearrange("p (g t) o -> p g o t", t=PACK)
+            if e >= E:
+                return
+            w4_grouped[e] = work.tile(
+                [P, PASSES, O2, PACK], BF16, name="w4_grouped", bufs=1, align_bytes=64
             )
-            return w4_grouped
+            nc.vector.tensor_copy(
+                out=w4_grouped[e][:], in_=w4_rows[e][:].rearrange("p (g t) o -> p g o t", t=PACK)
+            )
 
-        def quantise_w4(e, w4_grouped):
+        def quantise_w4(e):
+            if e >= E:
+                return
             w4_codes[e] = codes.tile([P, PASSES, O2], U32, name="w4_codes", align_bytes=64)
             w4_scales[e] = codes.tile([P, PASSES, O2], U8, name="w4_scales", align_bytes=64)
             nc.vector.quantize_mx(
                 out=w4_codes[e][:].rearrange("p g o -> p (g o)").bitcast(FP8X4),
                 scales=w4_scales[e][:].rearrange("p g o -> p (g o)"),
-                in_=w4_grouped[:].rearrange("p g o t -> p (g o t)"),
+                in_=w4_grouped[e][:].rearrange("p g o t -> p (g o t)"),
             )
 
-        def transpose_h2(e):
-            h2_grouped[e] = work.tile(
-                [P, PASSES * B * PACK], BF16, name="h2_grouped", bufs=1, align_bytes=64
-            )
-            words_in = h2_rows[e][:].bitcast(F32)
+        def transpose_h2(e, half):
+            if e >= E:
+                return
+            if half == 0:
+                h2_grouped[e] = work.tile(
+                    [P, PASSES * B * PACK], BF16, name="h2_grouped", bufs=1, align_bytes=64
+                )
+            words_in = h2_rows[e][:].rearrange("p r k -> p (r k)").bitcast(F32)
             words_out = h2_grouped[e][:].bitcast(F32).rearrange(
                 "p (g c u) -> p g c u", g=PASSES, u=2
             )
             blocks = H // 2 // P
-            for r in range(ROW_TILES):
+            lo, hi = bounds_of(half)
+            for r in range(lo // P, hi // P):
                 flipped = psum.tile([P, blocks, P], F32, name="flipped")
                 for j in range(blocks):
                     w0 = (r * blocks + j) * P
@@ -122,10 +139,13 @@ def tile_ensembledynamicsmodel_pa_t_kernel(
                     in_=flipped[:].rearrange("p (g u) c -> p g c u", u=2),
                 )
 
-        def quantise_h2(e):
-            h2_codes[e] = codes.tile([P, PASSES, B], U32, name="h2_codes", align_bytes=64)
-            h2_scales[e] = codes.tile([P, PASSES, B], U8, name="h2_scales", align_bytes=64)
-            for c0, c1 in COLUMN_CHUNKS:
+        def quantise_h2(e, half):
+            if e >= E:
+                return
+            if half == 0:
+                h2_codes[e] = codes.tile([P, PASSES, B], U32, name="h2_codes", align_bytes=64)
+                h2_scales[e] = codes.tile([P, PASSES, B], U8, name="h2_scales", align_bytes=64)
+            for c0, c1 in COLUMN_HALVES[half]:
                 for g in range(PASSES):
                     nc.vector.quantize_mx(
                         out=h2_codes[e][:, g, c0:c1].bitcast(FP8X4),
@@ -133,17 +153,17 @@ def tile_ensembledynamicsmodel_pa_t_kernel(
                         in_=h2_grouped[e][:, (g * B + c0) * PACK : (g * B + c1) * PACK],
                     )
 
-        def layer1(e, g_out):
-            h3_planes[e, g_out] = work.tile([P, PACK, B], BF16, name="h3_planes")
+        def layer1(e, half, g_out):
+            lo, hi = bounds_of(half)
+            planes = work.tile([P, PACK, hi - lo], BF16, name="h3_planes%d" % half)
+            h3_planes[e, half, g_out] = planes
             for t in range(PACK):
                 m = g_out * PACK + t
-                acc_wide = psum.tile([P, 512], F32, name="acc_wide")
-                acc_rest = psum.tile([P, 384], F32, name="acc_rest")
-                targets = (acc_wide[:, 0:512], acc_rest[:, 0:256], acc_rest[:, 256:384])
-                for (c0, c1), target in zip(COLUMN_CHUNKS, targets):
+                acc = psum.tile([P, hi - lo], F32, name="acc", bufs=4)
+                for c0, c1 in COLUMN_HALVES[half]:
                     for g in range(PASSES):
                         nc.tensor.matmul_mx(
-                            out=target,
+                            out=acc[:, c0 - lo : c1 - lo],
                             lhsT=w3_codes[e][:, g, m * P : (m + 1) * P].bitcast(FP8X4),
                             lhsT_scale=w3_scales[e][:, g, m * P : (m + 1) * P],
                             rhs=h2_codes[e][:, g, c0:c1].bitcast(FP8X4),
@@ -151,102 +171,163 @@ def tile_ensembledynamicsmodel_pa_t_kernel(
                             start=(g == 0),
                             stop=(g == PASSES - 1),
                         )
-                bias = b3_columns[:, e * (H // P) + m : e * (H // P) + m + 1]
                 nc.scalar.activation(
-                    out=h3_planes[e, g_out][:, t, 0:512], in_=acc_wide[:], func=ACT.Silu, bias=bias
-                )
-                nc.scalar.activation(
-                    out=h3_planes[e, g_out][:, t, 512:B], in_=acc_rest[:], func=ACT.Silu, bias=bias
+                    out=planes[:, t, :],
+                    in_=acc[:],
+                    func=ACT.Silu,
+                    bias=b3_columns[:, e * FEATURE_TILES + m : e * FEATURE_TILES + m + 1],
                 )
 
-        def quantise_h3(e, g_out):
-            if g_out == 0:
+        def regroup_h3(e, half, g_out):
+            lo, hi = bounds_of(half)
+            grouped = work.tile(
+                [P, hi - lo, PACK], BF16, name="h3_grouped%d" % half, align_bytes=64
+            )
+            h3_grouped[e, half, g_out] = grouped
+            interleave(nc.vector.tensor_copy, grouped[:], h3_planes[e, half, g_out][:])
+
+        def quantise_h3(e, half, g_out):
+            if half == 0 and g_out == 0:
                 h3_codes[e] = codes.tile([P, PASSES, B], U32, name="h3_codes", align_bytes=64)
                 h3_scales[e] = codes.tile([P, PASSES, B], U8, name="h3_scales", align_bytes=64)
-            h3_grouped = work.tile([P, B, PACK], BF16, name="h3_grouped", align_bytes=64)
-            for c0, c1 in COLUMN_CHUNKS:
-                interleave(
-                    nc.vector.tensor_copy, h3_grouped[:, c0:c1, :], h3_planes[e, g_out][:, :, c0:c1]
-                )
-            for c0, c1 in COLUMN_CHUNKS:
+            lo, hi = bounds_of(half)
+            for c0, c1 in COLUMN_HALVES[half]:
                 nc.vector.quantize_mx(
                     out=h3_codes[e][:, g_out, c0:c1].bitcast(FP8X4),
                     scales=h3_scales[e][:, g_out, c0:c1],
-                    in_=h3_grouped[:, c0:c1, :].rearrange("p c t -> p (c t)"),
+                    in_=h3_grouped[e, half, g_out][:, c0 - lo : c1 - lo, :].rearrange(
+                        "p c t -> p (c t)"
+                    ),
                 )
 
-        def layer2(e):
-            offset = work.tile([P, O], F32, name="offset")
+        def layer2_products(e, half):
+            lo, hi = bounds_of(half)
+            acc_out[e, half] = psum.tile([P, BANK_COLUMNS // O2, O2], F32, name="acc_out")
+            for r in range(lo // P, hi // P):
+                for g in range(PASSES):
+                    nc.tensor.matmul_mx(
+                        out=acc_out[e, half][:, r - lo // P, :],
+                        lhsT=h3_codes[e][:, g, r * P : (r + 1) * P].bitcast(FP8X4),
+                        lhsT_scale=h3_scales[e][:, g, r * P : (r + 1) * P],
+                        rhs=w4_codes[e][:, g, :].bitcast(FP8X4),
+                        rhs_scale=w4_scales[e][:, g, :],
+                        start=(g == 0),
+                        stop=(g == PASSES - 1),
+                    )
+
+        def layer2_outputs(e, half):
+            lo, hi = bounds_of(half)
+            r0, count = lo // P, (hi - lo) // P
+            if half == 0:
+                mean[e] = work.tile([P, ROW_TILES, O], F32, name="mean")
+                above[e] = work.tile([P, ROW_TILES, O], F32, name="above")
+                offset[e] = work.tile([P, O], F32, name="offset")
+                nc.vector.tensor_tensor(
+                    out=offset[e][:], in0=max_rows[:], in1=b4_rows[:, e, O:O2], op=ALU.subtract
+                )
             nc.vector.tensor_tensor(
-                out=offset[:], in0=max_rows[:], in1=b4_rows[:, e, O:O2], op=ALU.subtract
+                out=mean[e][:, r0 : r0 + count, :],
+                in0=acc_out[e, half][:, 0:count, 0:O],
+                in1=b4_rows[:, e, 0:O].unsqueeze(1).to_broadcast([P, count, O]),
+                op=ALU.add,
             )
-            mean = work.tile([P, ROW_TILES, O], F32, name="mean")
-            for r0 in range(0, ROW_TILES, ROW_TILES_PER_BANK):
-                count = min(ROW_TILES_PER_BANK, ROW_TILES - r0)
-                acc_out = psum.tile([P, ROW_TILES_PER_BANK, O2], F32, name="acc_out")
-                for r in range(r0, r0 + count):
-                    for g in range(PASSES):
-                        nc.tensor.matmul_mx(
-                            out=acc_out[:, r - r0, :],
-                            lhsT=h3_codes[e][:, g, r * P : (r + 1) * P].bitcast(FP8X4),
-                            lhsT_scale=h3_scales[e][:, g, r * P : (r + 1) * P],
-                            rhs=w4_codes[e][:, g, :].bitcast(FP8X4),
-                            rhs_scale=w4_scales[e][:, g, :],
-                            start=(g == 0),
-                            stop=(g == PASSES - 1),
-                        )
-                nc.vector.tensor_tensor(
-                    out=mean[:, r0 : r0 + count, :],
-                    in0=acc_out[:, 0:count, 0:O],
-                    in1=b4_rows[:, e, 0:O].unsqueeze(1).to_broadcast([P, count, O]),
-                    op=ALU.add,
-                )
-                nc.vector.tensor_tensor(
-                    out=above[:, e, r0 : r0 + count, :],
-                    in0=offset[:].unsqueeze(1).to_broadcast([P, count, O]),
-                    in1=acc_out[:, 0:count, O2 - O : O2],
-                    op=ALU.subtract,
-                )
-            nc.sync.dma_start(
-                out=out_0[e].rearrange("(p r) o -> p r o", r=ROW_TILES), in_=mean[:]
+            nc.vector.tensor_tensor(
+                out=above[e][:, r0 : r0 + count, :],
+                in0=offset[e][:].unsqueeze(1).to_broadcast([P, count, O]),
+                in1=acc_out[e, half][:, 0:count, O:O2],
+                op=ALU.subtract,
             )
+            if half == 1:
+                nc.sync.dma_start(
+                    out=out_0[e].rearrange("(p r) o -> p r o", r=ROW_TILES), in_=mean[e][:]
+                )
 
-        def flat(tile_of_members, e):
-            return tile_of_members[:, e].rearrange("p r o -> p (r o)")
+        def flat(rows):
+            return rows.rearrange("p r o -> p (r o)")
 
         def over_rows(row):
             return row.unsqueeze(1).to_broadcast([P, ROW_TILES, O])
 
-        def magnitude_on_scalar(members):
-            for e in members:
-                nc.scalar.activation(out=flat(soft, e), in_=flat(above, e), func=ACT.Abs)
+        def bounds_minus_w(e):
+            if e < 0:
+                return
+            nc.vector.scalar_tensor_tensor(
+                out=clamp[:, e],
+                in0=above[e][:],
+                scalar=0.0,
+                in1=over_rows(span[:]),
+                op0=ALU.max,
+                op1=ALU.subtract,
+            )
 
-        def tanh_of_half(members):
-            for e in members:
-                nc.scalar.activation(out=flat(soft, e), in_=flat(soft, e), func=ACT.Tanh, scale=0.5)
+        def bounds_tanh(e):
+            if e < 0:
+                return
+            tanh_above[e] = work.tile([P, ROW_TILES, O], F32, name="tanh_above")
+            tanh_w[e] = work.tile([P, ROW_TILES, O], F32, name="tanh_w")
+            nc.scalar.activation(out=flat(tanh_above[e][:]), in_=flat(above[e][:]), func=ACT.Abs)
+            nc.scalar.activation(
+                out=flat(tanh_w[e][:]), in_=flat(clamp[:, e]), func=ACT.Tanh, scale=-0.5
+            )
+            nc.scalar.activation(
+                out=flat(tanh_above[e][:]), in_=flat(tanh_above[e][:]), func=ACT.Tanh, scale=0.5
+            )
+            nc.scalar.activation(out=flat(tanh_w_size[:, e]), in_=flat(tanh_w[e][:]), func=ACT.Abs)
 
-        def log_sigmoid(members):
-            for e in members:
-                nc.scalar.activation(
-                    out=flat(soft, e), in_=flat(soft, e), func=ACT.Ln, scale=0.5, bias=half[:]
-                )
+        def bounds_clamp(e):
+            if e < 0:
+                return
+            nc.vector.scalar_tensor_tensor(
+                out=clamp[:, e],
+                in0=clamp[:, e],
+                scalar=0.0,
+                in1=over_rows(min_rows[:]),
+                op0=ALU.min,
+                op1=ALU.subtract,
+            )
 
-        def hard_part_of_first_bound(members):
-            for e in members:
-                nc.vector.scalar_tensor_tensor(
-                    out=hard[:, e],
-                    in0=above[:, e],
-                    scalar=0.0,
-                    in1=over_rows(span[:]),
-                    op0=ALU.max,
-                    op1=ALU.subtract,
-                )
+        def bounds_product(e):
+            if e < 0:
+                return
+            nc.vector.tensor_scalar(
+                out=tanh_above[e][:],
+                in0=tanh_above[e][:],
+                scalar1=-1.0,
+                scalar2=1.0,
+                op0=ALU.mult,
+                op1=ALU.add,
+            )
+            nc.vector.scalar_tensor_tensor(
+                out=product[:, e],
+                in0=tanh_w[e][:],
+                scalar=1.0,
+                in1=tanh_above[e][:],
+                op0=ALU.add,
+                op1=ALU.mult,
+            )
+
+        ident_words = consts.tile([P, P], F32)
+        make_identity(nc, ident_words[:])
+        ident_bf16 = consts.tile([P, P], BF16)
+        make_identity(nc, ident_bf16[:])
+        half_column = consts.tile([P, 1], F32)
+        nc.vector.memset(half_column[:], 0.5)
+        one_column = consts.tile([P, 1], F32)
+        nc.vector.memset(one_column[:], 1.0)
+        table_warmer = consts.tile([P, 1], F32)
+        nc.scalar.activation(out=table_warmer[:], in_=one_column[:], func=ACT.Silu)
+
+        b3_rows = consts.tile([P, P], BF16)
+        nc.vector.memset(b3_rows[:], 0.0)
+        nc.sync.dma_start(
+            out=b3_rows[0 : E * FEATURE_TILES, :], in_=b3.rearrange("e a (m p) -> (e a m) p", p=P)
+        )
+        b3_flipped = psum.tile([P, P], BF16, name="b3_flipped", tag="flipped")
+        nc.tensor.transpose(b3_flipped[:], b3_rows[:], ident_bf16[:])
+        b3_columns = consts.tile([P, E * FEATURE_TILES], F32)
+        nc.vector.tensor_copy(out=b3_columns[:], in_=b3_flipped[:, 0 : E * FEATURE_TILES])
 
         load(0)
-        nc.sync.dma_start(
-            out=b3_rows[0 : E * (H // P), :], in_=b3.rearrange("e a (m p) -> (e a m) p", p=P)
-        )
-        load(1)
         b4_rows = consts.tile([P, E, O2], BF16)
         nc.sync.dma_start(
             out=b4_rows[:].rearrange("p e o -> p (e o)"),
@@ -260,80 +341,76 @@ def tile_ensembledynamicsmodel_pa_t_kernel(
         nc.sync.dma_start(
             out=min_rows[:], in_=min_logvar.rearrange("a o -> (a o)").partition_broadcast(P)
         )
-
-        above = consts.tile([P, E, ROW_TILES, O], F32)
-        hard = consts.tile([P, E, ROW_TILES, O], F32)
-        soft = consts.tile([P, E, ROW_TILES, O], F32)
+        load(1)
         span = consts.tile([P, O], F32)
+        clamp = consts.tile([P, E, ROW_TILES, O], F32)
+        product = consts.tile([P, E, ROW_TILES, O], F32)
+        tanh_w_size = consts.tile([P, E, ROW_TILES, O], F32)
 
         quantise_w3(0)
-        transpose_h2(0)
-        w4_grouped = regroup_w4(0)
-        quantise_h2(0)
-        quantise_w4(0, w4_grouped)
-        b3_flipped = psum.tile([P, P], BF16, name="b3_flipped", tag="flipped")
-        nc.tensor.transpose(b3_flipped[:], b3_rows[:], ident_bf16[:])
-        b3_columns = consts.tile([P, E * (H // P)], F32)
-        nc.vector.tensor_copy(out=b3_columns[:], in_=b3_flipped[:, 0 : E * (H // P)])
+        transpose_h2(0, 0)
+        transpose_h2(0, 1)
+        quantise_h2(0, 0)
+        regroup_w4(0)
+        quantise_h2(0, 1)
+        quantise_w4(0)
+        nc.vector.tensor_tensor(out=span[:], in0=max_rows[:], in1=min_rows[:], op=ALU.subtract)
 
         for e in range(E):
-            if e + 2 < E:
-                load(e + 2)
-            if e + 1 < E:
-                quantise_w3(e + 1)
-            layer1(e, 0)
-            if e + 1 < E:
-                w4_grouped = regroup_w4(e + 1)
-            quantise_h3(e, 0)
-            if e + 1 < E:
-                quantise_w4(e + 1, w4_grouped)
-            layer1(e, 1)
-            if e + 1 < E:
-                transpose_h2(e + 1)
-            else:
-                nc.vector.tensor_tensor(
-                    out=span[:], in0=max_rows[:], in1=min_rows[:], op=ALU.subtract
-                )
-                magnitude_on_scalar(range(E - 1))
-                tanh_of_half(range(E - 1))
-                hard_part_of_first_bound(range(E - 1))
-            quantise_h3(e, 1)
-            if e + 1 < E:
-                quantise_h2(e + 1)
-            layer2(e)
+            load(e + 2)
+            bounds_minus_w(e - 1)
+            quantise_w3(e + 1)
+            layer1(e, 0, 0)
+            regroup_h3(e, 0, 0)
+            regroup_w4(e + 1)
+            quantise_h3(e, 0, 0)
+            layer1(e, 0, 1)
+            bounds_tanh(e - 1)
+            regroup_h3(e, 0, 1)
+            quantise_w4(e + 1)
+            quantise_h3(e, 0, 1)
+            layer1(e, 1, 0)
+            regroup_h3(e, 1, 0)
+            bounds_clamp(e - 1)
+            quantise_h3(e, 1, 0)
+            layer1(e, 1, 1)
+            layer2_products(e, 0)
+            transpose_h2(e + 1, 0)
+            transpose_h2(e + 1, 1)
+            bounds_product(e - 1)
+            regroup_h3(e, 1, 1)
+            layer2_outputs(e, 0)
+            quantise_h3(e, 1, 1)
+            quantise_h2(e + 1, 0)
+            quantise_h2(e + 1, 1)
+            layer2_products(e, 1)
+            layer2_outputs(e, 1)
 
-        magnitude_on_scalar([E - 1])
-        tanh_of_half([E - 1])
-        hard_part_of_first_bound([E - 1])
-        log_sigmoid(range(E))
+        bounds_minus_w(E - 1)
+        bounds_tanh(E - 1)
+        bounds_clamp(E - 1)
+        bounds_product(E - 1)
         for e in range(E):
+            nc.scalar.activation(
+                out=flat(product[:, e]),
+                in_=flat(product[:, e]),
+                func=ACT.Ln,
+                scale=-0.25,
+                bias=one_column[:],
+            )
+            nc.scalar.activation(
+                out=flat(tanh_w_size[:, e]),
+                in_=flat(tanh_w_size[:, e]),
+                func=ACT.Ln,
+                scale=0.5,
+                bias=half_column[:],
+            )
             nc.vector.tensor_tensor(
-                out=above[:, e], in0=soft[:, e], in1=hard[:, e], op=ALU.subtract
+                out=product[:, e], in0=product[:, e], in1=clamp[:, e], op=ALU.subtract
             )
-        for e in range(E):
-            nc.vector.scalar_tensor_tensor(
-                out=soft[:, e],
-                in0=above[:, e],
-                scalar=-1.0,
-                in1=above[:, e],
-                op0=ALU.mult,
-                op1=ALU.max,
-            )
-        for e in range(E):
-            nc.vector.scalar_tensor_tensor(
-                out=hard[:, e],
-                in0=above[:, e],
-                scalar=0.0,
-                in1=over_rows(min_rows[:]),
-                op0=ALU.max,
-                op1=ALU.add,
-            )
-        tanh_of_half(range(E))
-        log_sigmoid(range(E))
-        for e in range(E):
             nc.vector.tensor_tensor(
-                out=above[:, e], in0=hard[:, e], in1=soft[:, e], op=ALU.subtract
+                out=product[:, e], in0=product[:, e], in1=tanh_w_size[:, e], op=ALU.subtract
             )
             nc.sync.dma_start(
-                out=out_1[e].rearrange("(p r) o -> p r o", r=ROW_TILES), in_=above[:, e]
+                out=out_1[e].rearrange("(p r) o -> p r o", r=ROW_TILES), in_=product[:, e]
             )

@@ -20,6 +20,7 @@ FEATURE_TILES = H // P
 W3_CHUNK = 512
 COLUMN_HALVES = (((0, 512),), ((512, 768), (768, 896)))
 BANK_COLUMNS = 512
+BANKS = 6
 
 FLOPS = 2 * E * B * H * (H + O2)
 
@@ -86,7 +87,7 @@ def tile_ensembledynamicsmodel_pa_t_kernel(
                         [P, W3_CHUNK, PACK], BF16, name="w3_grouped", bufs=4, align_bytes=64
                     )
                     grouped.append(w3_grouped)
-                    copy = nc.scalar.copy if (n0 > 0 and g == 0) else nc.vector.tensor_copy
+                    copy = nc.scalar.copy if n0 > 0 else nc.vector.tensor_copy
                     interleave(copy, w3_grouped[:], w3_rows[e][:, g, :, n0 : n0 + W3_CHUNK])
                 for g in range(PASSES):
                     nc.vector.quantize_mx(
@@ -130,7 +131,7 @@ def tile_ensembledynamicsmodel_pa_t_kernel(
             blocks = H // 2 // P
             lo, hi = bounds_of(half)
             for r in range(lo // P, hi // P):
-                flipped = psum.tile([P, blocks, P], F32, name="flipped")
+                flipped = psum.tile([P, blocks, P], F32, name="flipped", tag="bank", bufs=BANKS)
                 for j in range(blocks):
                     w0 = (r * blocks + j) * P
                     nc.tensor.transpose(flipped[:, j, :], words_in[:, w0 : w0 + P], ident_words[:])
@@ -159,7 +160,7 @@ def tile_ensembledynamicsmodel_pa_t_kernel(
             h3_planes[e, half, g_out] = planes
             for t in range(PACK):
                 m = g_out * PACK + t
-                acc = psum.tile([P, hi - lo], F32, name="acc", bufs=4)
+                acc = psum.tile([P, hi - lo], F32, name="acc", tag="bank", bufs=BANKS)
                 for c0, c1 in COLUMN_HALVES[half]:
                     for g in range(PASSES):
                         nc.tensor.matmul_mx(
@@ -322,7 +323,7 @@ def tile_ensembledynamicsmodel_pa_t_kernel(
         nc.sync.dma_start(
             out=b3_rows[0 : E * FEATURE_TILES, :], in_=b3.rearrange("e a (m p) -> (e a m) p", p=P)
         )
-        b3_flipped = psum.tile([P, P], BF16, name="b3_flipped", tag="flipped")
+        b3_flipped = psum.tile([P, P], BF16, name="b3_flipped", tag="bank", bufs=BANKS)
         nc.tensor.transpose(b3_flipped[:], b3_rows[:], ident_bf16[:])
         b3_columns = consts.tile([P, E * FEATURE_TILES], F32)
         nc.vector.tensor_copy(out=b3_columns[:], in_=b3_flipped[:, 0 : E * FEATURE_TILES])
@@ -374,14 +375,14 @@ def tile_ensembledynamicsmodel_pa_t_kernel(
             bounds_clamp(e - 1)
             quantise_h3(e, 1, 0)
             layer1(e, 1, 1)
-            layer2_products(e, 0)
             transpose_h2(e + 1, 0)
             transpose_h2(e + 1, 1)
-            bounds_product(e - 1)
             regroup_h3(e, 1, 1)
-            layer2_outputs(e, 0)
+            bounds_product(e - 1)
             quantise_h3(e, 1, 1)
             quantise_h2(e + 1, 0)
+            layer2_products(e, 0)
+            layer2_outputs(e, 0)
             quantise_h2(e + 1, 1)
             layer2_products(e, 1)
             layer2_outputs(e, 1)

@@ -21,6 +21,8 @@ W3_CHUNK = 512
 COLUMN_HALVES = (((0, 512),), ((512, 768), (768, 896)))
 BANK_COLUMNS = 512
 BANKS = 6
+ALL_ROWS = slice(0, ROW_TILES)
+HALF_ROWS = (slice(0, 4), slice(4, ROW_TILES))
 
 FLOPS = 2 * E * B * H * (H + O2)
 
@@ -246,63 +248,71 @@ def tile_ensembledynamicsmodel_pa_t_kernel(
         def flat(rows):
             return rows.rearrange("p r o -> p (r o)")
 
-        def over_rows(row):
-            return row.unsqueeze(1).to_broadcast([P, ROW_TILES, O])
+        def over(row, rows):
+            return row.unsqueeze(1).to_broadcast([P, rows.stop - rows.start, O])
 
-        def bounds_minus_w(e):
+        def bounds_minus_w(e, rows=ALL_ROWS):
             if e < 0:
                 return
             nc.vector.scalar_tensor_tensor(
-                out=clamp[:, e],
-                in0=above[e][:],
+                out=clamp[:, e, rows],
+                in0=above[e][:, rows],
                 scalar=0.0,
-                in1=over_rows(span[:]),
+                in1=over(span[:], rows),
                 op0=ALU.max,
                 op1=ALU.subtract,
             )
 
-        def bounds_tanh(e):
+        def bounds_tanh(e, rows=ALL_ROWS):
             if e < 0:
                 return
-            tanh_above[e] = work.tile([P, ROW_TILES, O], F32, name="tanh_above")
-            tanh_w[e] = work.tile([P, ROW_TILES, O], F32, name="tanh_w")
-            nc.scalar.activation(out=flat(tanh_above[e][:]), in_=flat(above[e][:]), func=ACT.Abs)
+            if rows.start == 0:
+                tanh_above[e] = work.tile([P, ROW_TILES, O], F32, name="tanh_above")
+                tanh_w[e] = work.tile([P, ROW_TILES, O], F32, name="tanh_w")
             nc.scalar.activation(
-                out=flat(tanh_w[e][:]), in_=flat(clamp[:, e]), func=ACT.Tanh, scale=-0.5
+                out=flat(tanh_above[e][:, rows]), in_=flat(above[e][:, rows]), func=ACT.Abs
             )
             nc.scalar.activation(
-                out=flat(tanh_above[e][:]), in_=flat(tanh_above[e][:]), func=ACT.Tanh, scale=0.5
+                out=flat(tanh_w[e][:, rows]), in_=flat(clamp[:, e, rows]), func=ACT.Tanh, scale=-0.5
             )
-            nc.scalar.activation(out=flat(tanh_w_size[:, e]), in_=flat(tanh_w[e][:]), func=ACT.Abs)
+            nc.scalar.activation(
+                out=flat(tanh_above[e][:, rows]),
+                in_=flat(tanh_above[e][:, rows]),
+                func=ACT.Tanh,
+                scale=0.5,
+            )
+            nc.scalar.activation(
+                out=flat(tanh_w_size[:, e, rows]), in_=flat(tanh_w[e][:, rows]), func=ACT.Abs
+            )
 
-        def bounds_clamp(e):
+        def bounds_clamp(e, rows=ALL_ROWS):
             if e < 0:
                 return
             nc.vector.scalar_tensor_tensor(
-                out=clamp[:, e],
-                in0=clamp[:, e],
+                out=clamp[:, e, rows],
+                in0=clamp[:, e, rows],
                 scalar=0.0,
-                in1=over_rows(min_rows[:]),
+                in1=over(min_rows[:], rows),
                 op0=ALU.min,
                 op1=ALU.subtract,
             )
 
-        def bounds_product(e):
+        def bounds_product(e, rows=ALL_ROWS):
             if e < 0:
                 return
             nc.vector.tensor_scalar(
-                out=tanh_above[e][:],
-                in0=tanh_above[e][:],
+                out=tanh_above[e][:, rows],
+                in0=tanh_above[e][:, rows],
                 scalar1=-1.0,
                 scalar2=1.0,
                 op0=ALU.mult,
                 op1=ALU.add,
             )
             nc.vector.scalar_tensor_tensor(
-                out=product[:, e],
-                in0=tanh_w[e][:],
+                out=product[:, e, rows],
+                in0=tanh_w[e][:, rows],
                 scalar=1.0,
-                in1=tanh_above[e][:],
+                in1=tanh_above[e][:, rows],
                 op0=ALU.add,
                 op1=ALU.mult,
             )
@@ -357,7 +367,7 @@ def tile_ensembledynamicsmodel_pa_t_kernel(
         quantise_w4(0)
         nc.vector.tensor_tensor(out=span[:], in0=max_rows[:], in1=min_rows[:], op=ALU.subtract)
 
-        for e in range(E):
+        for e in range(E - 1):
             load(e + 2)
             bounds_minus_w(e - 1)
             quantise_w3(e + 1)
@@ -387,10 +397,35 @@ def tile_ensembledynamicsmodel_pa_t_kernel(
             layer2_products(e, 1)
             layer2_outputs(e, 1)
 
-        bounds_minus_w(E - 1)
-        bounds_tanh(E - 1)
-        bounds_clamp(E - 1)
-        bounds_product(E - 1)
+        e = E - 1
+        layer1(e, 0, 0)
+        regroup_h3(e, 0, 0)
+        bounds_minus_w(e - 1)
+        quantise_h3(e, 0, 0)
+        layer1(e, 0, 1)
+        regroup_h3(e, 0, 1)
+        quantise_h3(e, 0, 1)
+        layer1(e, 1, 0)
+        layer1(e, 1, 1)
+        layer2_products(e, 0)
+        regroup_h3(e, 1, 0)
+        layer2_outputs(e, 0)
+        quantise_h3(e, 1, 0)
+        regroup_h3(e, 1, 1)
+        bounds_minus_w(e, HALF_ROWS[0])
+        quantise_h3(e, 1, 1)
+        bounds_tanh(e - 1)
+        bounds_tanh(e, HALF_ROWS[0])
+        layer2_products(e, 1)
+        layer2_outputs(e, 1)
+        bounds_minus_w(e, HALF_ROWS[1])
+        bounds_tanh(e, HALF_ROWS[1])
+        bounds_clamp(e - 1)
+        bounds_product(e - 1)
+        bounds_clamp(e, HALF_ROWS[0])
+        bounds_product(e, HALF_ROWS[0])
+        bounds_clamp(e, HALF_ROWS[1])
+        bounds_product(e, HALF_ROWS[1])
         for e in range(E):
             nc.scalar.activation(
                 out=flat(product[:, e]),

@@ -18,6 +18,7 @@ PASSES = H // K_PASS
 ROW_TILES = B // P
 FEATURE_TILES = H // P
 W3_CHUNK = 512
+SCALAR_COLUMNS = 384
 COLUMN_HALVES = (((0, 512),), ((512, 768), (768, 896)))
 BANK_COLUMNS = 512
 BANKS = 6
@@ -82,20 +83,31 @@ def tile_ensembledynamicsmodel_pa_t_kernel(
                 return
             w3_codes[e] = codes.tile([P, PASSES, H], U32, name="w3_codes", align_bytes=64)
             w3_scales[e] = codes.tile([P, PASSES, H], U8, name="w3_scales", align_bytes=64)
+            grouped = {}
             for n0 in range(0, H, W3_CHUNK):
-                grouped = []
                 for g in range(PASSES):
                     w3_grouped = work.tile(
                         [P, W3_CHUNK, PACK], BF16, name="w3_grouped", bufs=4, align_bytes=64
                     )
-                    grouped.append(w3_grouped)
-                    copy = nc.scalar.copy if n0 > 0 else nc.vector.tensor_copy
-                    interleave(copy, w3_grouped[:], w3_rows[e][:, g, :, n0 : n0 + W3_CHUNK])
+                    grouped[n0, g] = w3_grouped
+                    mine = W3_CHUNK if n0 == 0 else W3_CHUNK - SCALAR_COLUMNS
+                    interleave(
+                        nc.vector.tensor_copy,
+                        w3_grouped[:, 0:mine, :],
+                        w3_rows[e][:, g, :, n0 : n0 + mine],
+                    )
+                    if mine < W3_CHUNK:
+                        interleave(
+                            nc.scalar.copy,
+                            w3_grouped[:, mine:W3_CHUNK, :],
+                            w3_rows[e][:, g, :, n0 + mine : n0 + W3_CHUNK],
+                        )
+            for n0 in range(0, H, W3_CHUNK):
                 for g in range(PASSES):
                     nc.vector.quantize_mx(
                         out=w3_codes[e][:, g, n0 : n0 + W3_CHUNK].bitcast(FP8X4),
                         scales=w3_scales[e][:, g, n0 : n0 + W3_CHUNK],
-                        in_=grouped[g][:].rearrange("p n t -> p (n t)"),
+                        in_=grouped[n0, g][:].rearrange("p n t -> p (n t)"),
                     )
 
         def regroup_w4(e):

@@ -18,7 +18,7 @@ PASSES = H // K_PASS
 ROW_TILES = B // P
 FEATURE_TILES = H // P
 W3_CHUNK = 512
-SCALAR_COLUMNS = 384
+SCALAR_COLUMNS = (512, 384)
 COLUMN_HALVES = (((0, 512),), ((512, 768), (768, 896)))
 BANK_COLUMNS = 512
 BANKS = 6
@@ -90,12 +90,13 @@ def tile_ensembledynamicsmodel_pa_t_kernel(
                         [P, W3_CHUNK, PACK], BF16, name="w3_grouped", bufs=4, align_bytes=64
                     )
                     grouped[n0, g] = w3_grouped
-                    mine = W3_CHUNK if n0 == 0 else W3_CHUNK - SCALAR_COLUMNS
-                    interleave(
-                        nc.vector.tensor_copy,
-                        w3_grouped[:, 0:mine, :],
-                        w3_rows[e][:, g, :, n0 : n0 + mine],
-                    )
+                    mine = W3_CHUNK if n0 == 0 else W3_CHUNK - SCALAR_COLUMNS[g]
+                    if mine > 0:
+                        interleave(
+                            nc.vector.tensor_copy,
+                            w3_grouped[:, 0:mine, :],
+                            w3_rows[e][:, g, :, n0 : n0 + mine],
+                        )
                     if mine < W3_CHUNK:
                         interleave(
                             nc.scalar.copy,
@@ -309,7 +310,7 @@ def tile_ensembledynamicsmodel_pa_t_kernel(
                 op1=ALU.subtract,
             )
 
-        def bounds_product(e, rows=ALL_ROWS):
+        def bounds_one_minus(e, rows=ALL_ROWS):
             if e < 0:
                 return
             nc.vector.tensor_scalar(
@@ -320,6 +321,10 @@ def tile_ensembledynamicsmodel_pa_t_kernel(
                 op0=ALU.mult,
                 op1=ALU.add,
             )
+
+        def bounds_product(e, rows=ALL_ROWS):
+            if e < 0:
+                return
             nc.vector.scalar_tensor_tensor(
                 out=product[:, e, rows],
                 in0=tanh_w[e][:, rows],
@@ -329,6 +334,19 @@ def tile_ensembledynamicsmodel_pa_t_kernel(
                 op1=ALU.mult,
             )
 
+        def logarithm_of_size(e):
+            nc.scalar.activation(
+                out=flat(tanh_w_size[:, e]),
+                in_=flat(tanh_w_size[:, e]),
+                func=ACT.Ln,
+                scale=0.5,
+                bias=half_column[:],
+            )
+            nc.vector.tensor_tensor(
+                out=clamp[:, e], in0=clamp[:, e], in1=tanh_w_size[:, e], op=ALU.add
+            )
+
+        load(0)
         ident_words = consts.tile([P, P], F32)
         make_identity(nc, ident_words[:])
         ident_bf16 = consts.tile([P, P], BF16)
@@ -345,12 +363,7 @@ def tile_ensembledynamicsmodel_pa_t_kernel(
         nc.sync.dma_start(
             out=b3_rows[0 : E * FEATURE_TILES, :], in_=b3.rearrange("e a (m p) -> (e a m) p", p=P)
         )
-        b3_flipped = psum.tile([P, P], BF16, name="b3_flipped", tag="bank", bufs=BANKS)
-        nc.tensor.transpose(b3_flipped[:], b3_rows[:], ident_bf16[:])
-        b3_columns = consts.tile([P, E * FEATURE_TILES], F32)
-        nc.vector.tensor_copy(out=b3_columns[:], in_=b3_flipped[:, 0 : E * FEATURE_TILES])
 
-        load(0)
         b4_rows = consts.tile([P, E, O2], BF16)
         nc.sync.dma_start(
             out=b4_rows[:].rearrange("p e o -> p (e o)"),
@@ -373,10 +386,14 @@ def tile_ensembledynamicsmodel_pa_t_kernel(
         quantise_w3(0)
         transpose_h2(0, 0)
         transpose_h2(0, 1)
+        b3_flipped = psum.tile([P, P], BF16, name="b3_flipped", tag="bank", bufs=BANKS)
+        nc.tensor.transpose(b3_flipped[:], b3_rows[:], ident_bf16[:])
         quantise_h2(0, 0)
         regroup_w4(0)
         quantise_h2(0, 1)
         quantise_w4(0)
+        b3_columns = consts.tile([P, E * FEATURE_TILES], F32)
+        nc.vector.tensor_copy(out=b3_columns[:], in_=b3_flipped[:, 0 : E * FEATURE_TILES])
         nc.vector.tensor_tensor(out=span[:], in0=max_rows[:], in1=min_rows[:], op=ALU.subtract)
 
         for e in range(E - 1):
@@ -395,6 +412,7 @@ def tile_ensembledynamicsmodel_pa_t_kernel(
             layer1(e, 1, 0)
             regroup_h3(e, 1, 0)
             bounds_clamp(e - 1)
+            bounds_one_minus(e - 1)
             quantise_h3(e, 1, 0)
             layer1(e, 1, 1)
             transpose_h2(e + 1, 0)
@@ -433,32 +451,33 @@ def tile_ensembledynamicsmodel_pa_t_kernel(
         bounds_minus_w(e, HALF_ROWS[1])
         bounds_tanh(e, HALF_ROWS[1])
         bounds_clamp(e - 1)
-        bounds_product(e - 1)
+        bounds_one_minus(e - 1)
         bounds_clamp(e, HALF_ROWS[0])
-        bounds_product(e, HALF_ROWS[0])
+        bounds_product(e - 1)
+        bounds_one_minus(e, HALF_ROWS[0])
         bounds_clamp(e, HALF_ROWS[1])
+        bounds_product(e, HALF_ROWS[0])
+        bounds_one_minus(e, HALF_ROWS[1])
+        logarithm_of_size(0)
         bounds_product(e, HALF_ROWS[1])
         for e in range(E):
-            nc.scalar.activation(
-                out=flat(product[:, e]),
-                in_=flat(product[:, e]),
-                func=ACT.Ln,
-                scale=-0.25,
-                bias=one_column[:],
-            )
-            nc.scalar.activation(
-                out=flat(tanh_w_size[:, e]),
-                in_=flat(tanh_w_size[:, e]),
-                func=ACT.Ln,
-                scale=0.5,
-                bias=half_column[:],
-            )
-            nc.vector.tensor_tensor(
-                out=product[:, e], in0=product[:, e], in1=clamp[:, e], op=ALU.subtract
-            )
-            nc.vector.tensor_tensor(
-                out=product[:, e], in0=product[:, e], in1=tanh_w_size[:, e], op=ALU.subtract
-            )
-            nc.sync.dma_start(
-                out=out_1[e].rearrange("(p r) o -> p r o", r=ROW_TILES), in_=product[:, e]
-            )
+            if e > 0:
+                logarithm_of_size(e)
+            for rows in HALF_ROWS if e == E - 1 else (ALL_ROWS,):
+                nc.scalar.activation(
+                    out=flat(product[:, e, rows]),
+                    in_=flat(product[:, e, rows]),
+                    func=ACT.Ln,
+                    scale=-0.25,
+                    bias=one_column[:],
+                )
+                nc.vector.tensor_tensor(
+                    out=product[:, e, rows],
+                    in0=product[:, e, rows],
+                    in1=clamp[:, e, rows],
+                    op=ALU.subtract,
+                )
+                nc.sync.dma_start(
+                    out=out_1[e].rearrange("(p r) o -> p r o", r=ROW_TILES)[:, rows, :],
+                    in_=product[:, e, rows],
+                )

@@ -364,19 +364,15 @@ def tile_ensembledynamicsmodel_pa_t_kernel(
             out=b3_rows[0 : E * FEATURE_TILES, :], in_=b3.rearrange("e a (m p) -> (e a m) p", p=P)
         )
 
-        b4_rows = consts.tile([P, E, O2], BF16)
+        vectors = consts.tile([P, E * O2 + 2 * O], BF16)
+        nc.vector.memset(vectors[:], 0.0)
+        ones = consts.tile([P, P], BF16)
+        nc.vector.memset(ones[:], 1.0)
         nc.sync.dma_start(
-            out=b4_rows[:].rearrange("p e o -> p (e o)"),
-            in_=b4.rearrange("e a o -> (e a o)").partition_broadcast(P),
+            out=vectors[0:1, 0 : E * O2], in_=b4.rearrange("e a o -> (e a o)").unsqueeze(0)
         )
-        max_rows = consts.tile([P, O], BF16)
-        nc.sync.dma_start(
-            out=max_rows[:], in_=max_logvar.rearrange("a o -> (a o)").partition_broadcast(P)
-        )
-        min_rows = consts.tile([P, O], BF16)
-        nc.sync.dma_start(
-            out=min_rows[:], in_=min_logvar.rearrange("a o -> (a o)").partition_broadcast(P)
-        )
+        nc.sync.dma_start(out=vectors[0:1, E * O2 : E * O2 + O], in_=max_logvar)
+        nc.sync.dma_start(out=vectors[0:1, E * O2 + O : E * O2 + 2 * O], in_=min_logvar)
         load(1)
         span = consts.tile([P, O], F32)
         clamp = consts.tile([P, E, ROW_TILES, O], F32)
@@ -388,12 +384,28 @@ def tile_ensembledynamicsmodel_pa_t_kernel(
         transpose_h2(0, 1)
         b3_flipped = psum.tile([P, P], BF16, name="b3_flipped", tag="bank", bufs=BANKS)
         nc.tensor.transpose(b3_flipped[:], b3_rows[:], ident_bf16[:])
+        repeated = consts.tile([P, E * O2 + 2 * O], F32)
+        repeated_sums = {}
+        for c0 in range(0, E * O2 + 2 * O, BANK_COLUMNS):
+            c1 = min(c0 + BANK_COLUMNS, E * O2 + 2 * O)
+            repeated_sums[c0] = psum.tile(
+                [P, c1 - c0], F32, name="repeated_sums", tag="bank", bufs=BANKS
+            )
+            nc.tensor.matmul(
+                out=repeated_sums[c0][:], lhsT=ones[:], rhs=vectors[:, c0:c1], start=True, stop=True
+            )
+        b4_rows = repeated[:, 0 : E * O2].rearrange("p (e o) -> p e o", e=E)
+        max_rows = repeated[:, E * O2 : E * O2 + O]
+        min_rows = repeated[:, E * O2 + O : E * O2 + 2 * O]
         quantise_h2(0, 0)
         regroup_w4(0)
         quantise_h2(0, 1)
         quantise_w4(0)
         b3_columns = consts.tile([P, E * FEATURE_TILES], F32)
         nc.vector.tensor_copy(out=b3_columns[:], in_=b3_flipped[:, 0 : E * FEATURE_TILES])
+        for c0 in range(0, E * O2 + 2 * O, BANK_COLUMNS):
+            c1 = min(c0 + BANK_COLUMNS, E * O2 + 2 * O)
+            nc.vector.tensor_copy(out=repeated[:, c0:c1], in_=repeated_sums[c0][:])
         nc.vector.tensor_tensor(out=span[:], in0=max_rows[:], in1=min_rows[:], op=ALU.subtract)
 
         for e in range(E - 1):

@@ -53,20 +53,8 @@ def tile_ensembledynamicsmodel_pa_t_kernel(
         h3_planes, h3_grouped, h3_codes, h3_scales, w4_codes, w4_scales = {}, {}, {}, {}, {}, {}
         acc_out, mean, above, offset, tanh_above, tanh_w = {}, {}, {}, {}, {}, {}
 
-        def load(e):
-            if e >= E:
-                return
-            h2_rows[e] = loads.tile([P, ROW_TILES, H], BF16, name="h2_rows")
+        def load_w3(e):
             w3_rows[e] = loads.tile([P, PASSES, PACK, H], BF16, name="w3_rows")
-            w4_rows[e] = loads.tile([P, PASSES * PACK, O2], BF16, name="w4_rows")
-
-            def load_h2(half):
-                lo, hi = bounds_of(half)
-                nc.sync.dma_start(
-                    out=h2_rows[e][:, lo // P : hi // P, :],
-                    in_=h2[e].rearrange("(p r) k -> p r k", r=ROW_TILES)[:, lo // P : hi // P, :],
-                )
-
             for g in range(PASSES):
                 nc.sync.dma_start(
                     out=w3_rows[e][:, g].rearrange("p (u i) n -> p u (i n)", i=2),
@@ -74,8 +62,18 @@ def tile_ensembledynamicsmodel_pa_t_kernel(
                         "(u p i) n -> p u (i n)", u=2, i=2
                     ),
                 )
-            load_h2(0)
-            load_h2(1)
+
+        def load_h2(e):
+            h2_rows[e] = loads.tile([P, ROW_TILES, H], BF16, name="h2_rows")
+            for half in range(2):
+                lo, hi = bounds_of(half)
+                nc.sync.dma_start(
+                    out=h2_rows[e][:, lo // P : hi // P, :],
+                    in_=h2[e].rearrange("(p r) k -> p r k", r=ROW_TILES)[:, lo // P : hi // P, :],
+                )
+
+        def load_w4(e):
+            w4_rows[e] = loads.tile([P, PASSES * PACK, O2], BF16, name="w4_rows")
             nc.sync.dma_start(out=w4_rows[e][:], in_=w4[e].rearrange("(j p) o -> p j o", p=P))
 
         def quantise_w3(e):
@@ -346,7 +344,8 @@ def tile_ensembledynamicsmodel_pa_t_kernel(
                 out=clamp[:, e], in0=clamp[:, e], in1=tanh_w_size[:, e], op=ALU.add
             )
 
-        load(0)
+        load_w3(0)
+        load_h2(0)
         ident_words = consts.tile([P, P], F32)
         make_identity(nc, ident_words[:])
         ident_bf16 = consts.tile([P, P], BF16)
@@ -363,6 +362,8 @@ def tile_ensembledynamicsmodel_pa_t_kernel(
         nc.sync.dma_start(
             out=b3_rows[0 : E * FEATURE_TILES, :], in_=b3.rearrange("e a (m p) -> (e a m) p", p=P)
         )
+        load_w3(1)
+        load_w4(0)
 
         vectors = consts.tile([P, E * O2 + 2 * O], BF16)
         nc.vector.memset(vectors[:], 0.0)
@@ -373,7 +374,8 @@ def tile_ensembledynamicsmodel_pa_t_kernel(
         )
         nc.sync.dma_start(out=vectors[0:1, E * O2 : E * O2 + O], in_=max_logvar)
         nc.sync.dma_start(out=vectors[0:1, E * O2 + O : E * O2 + 2 * O], in_=min_logvar)
-        load(1)
+        load_h2(1)
+        load_w4(1)
         span = consts.tile([P, O], F32)
         clamp = consts.tile([P, E, ROW_TILES, O], F32)
         product = consts.tile([P, E, ROW_TILES, O], F32)
@@ -384,42 +386,41 @@ def tile_ensembledynamicsmodel_pa_t_kernel(
         transpose_h2(0, 1)
         b3_flipped = psum.tile([P, P], BF16, name="b3_flipped", tag="bank", bufs=BANKS)
         nc.tensor.transpose(b3_flipped[:], b3_rows[:], ident_bf16[:])
+        quantise_h2(0, 0)
+        quantise_h2(0, 1)
+        b3_columns = consts.tile([P, E * FEATURE_TILES], F32)
+        nc.vector.tensor_copy(out=b3_columns[:], in_=b3_flipped[:, 0 : E * FEATURE_TILES])
         repeated = consts.tile([P, E * O2 + 2 * O], F32)
-        repeated_sums = {}
-        for c0 in range(0, E * O2 + 2 * O, BANK_COLUMNS):
-            c1 = min(c0 + BANK_COLUMNS, E * O2 + 2 * O)
-            repeated_sums[c0] = psum.tile(
-                [P, c1 - c0], F32, name="repeated_sums", tag="bank", bufs=BANKS
-            )
-            nc.tensor.matmul(
-                out=repeated_sums[c0][:], lhsT=ones[:], rhs=vectors[:, c0:c1], start=True, stop=True
-            )
         b4_rows = repeated[:, 0 : E * O2].rearrange("p (e o) -> p e o", e=E)
         max_rows = repeated[:, E * O2 : E * O2 + O]
         min_rows = repeated[:, E * O2 + O : E * O2 + 2 * O]
-        quantise_h2(0, 0)
-        regroup_w4(0)
-        quantise_h2(0, 1)
-        quantise_w4(0)
-        b3_columns = consts.tile([P, E * FEATURE_TILES], F32)
-        nc.vector.tensor_copy(out=b3_columns[:], in_=b3_flipped[:, 0 : E * FEATURE_TILES])
-        for c0 in range(0, E * O2 + 2 * O, BANK_COLUMNS):
-            c1 = min(c0 + BANK_COLUMNS, E * O2 + 2 * O)
-            nc.vector.tensor_copy(out=repeated[:, c0:c1], in_=repeated_sums[c0][:])
-        nc.vector.tensor_tensor(out=span[:], in0=max_rows[:], in1=min_rows[:], op=ALU.subtract)
+
+        def repeat_vectors():
+            for c0 in range(0, E * O2 + 2 * O, BANK_COLUMNS):
+                c1 = min(c0 + BANK_COLUMNS, E * O2 + 2 * O)
+                sums = psum.tile([P, c1 - c0], F32, name="sums", tag="bank", bufs=BANKS)
+                nc.tensor.matmul(
+                    out=sums[:], lhsT=ones[:], rhs=vectors[:, c0:c1], start=True, stop=True
+                )
+                nc.vector.tensor_copy(out=repeated[:, c0:c1], in_=sums[:])
+            nc.vector.tensor_tensor(out=span[:], in0=max_rows[:], in1=min_rows[:], op=ALU.subtract)
 
         for e in range(E - 1):
-            load(e + 2)
+            if e + 2 < E:
+                load_w3(e + 2)
+                load_h2(e + 2)
             bounds_minus_w(e - 1)
             quantise_w3(e + 1)
             layer1(e, 0, 0)
             regroup_h3(e, 0, 0)
-            regroup_w4(e + 1)
+            regroup_w4(e)
             quantise_h3(e, 0, 0)
+            if e + 2 < E:
+                load_w4(e + 2)
             layer1(e, 0, 1)
             bounds_tanh(e - 1)
             regroup_h3(e, 0, 1)
-            quantise_w4(e + 1)
+            quantise_w4(e)
             quantise_h3(e, 0, 1)
             layer1(e, 1, 0)
             regroup_h3(e, 1, 0)
@@ -427,6 +428,8 @@ def tile_ensembledynamicsmodel_pa_t_kernel(
             bounds_one_minus(e - 1)
             quantise_h3(e, 1, 0)
             layer1(e, 1, 1)
+            if e == 0:
+                repeat_vectors()
             transpose_h2(e + 1, 0)
             transpose_h2(e + 1, 1)
             regroup_h3(e, 1, 1)
@@ -443,9 +446,11 @@ def tile_ensembledynamicsmodel_pa_t_kernel(
         layer1(e, 0, 0)
         regroup_h3(e, 0, 0)
         bounds_minus_w(e - 1)
+        regroup_w4(e)
         quantise_h3(e, 0, 0)
         layer1(e, 0, 1)
         regroup_h3(e, 0, 1)
+        quantise_w4(e)
         quantise_h3(e, 0, 1)
         layer1(e, 1, 0)
         layer1(e, 1, 1)

@@ -51,17 +51,17 @@ def tile_ensembledynamicsmodel_pa_t_kernel(
         w3_rows, h2_rows, w4_rows, w4_grouped = {}, {}, {}, {}
         w3_codes, w3_scales, h2_grouped, h2_codes, h2_scales = {}, {}, {}, {}, {}
         h3_planes, h3_grouped, h3_codes, h3_scales, w4_codes, w4_scales = {}, {}, {}, {}, {}, {}
-        acc_out, mean, above, offset, tanh_above, tanh_w = {}, {}, {}, {}, {}, {}
+        acc_out, outputs, tanh_above, tanh_w = {}, {}, {}, {}
 
-        def load_w3(e):
-            w3_rows[e] = loads.tile([P, PASSES, PACK, H], BF16, name="w3_rows")
-            for g in range(PASSES):
-                nc.sync.dma_start(
-                    out=w3_rows[e][:, g].rearrange("p (u i) n -> p u (i n)", i=2),
-                    in_=w3[e, g * K_PASS : (g + 1) * K_PASS, :].rearrange(
-                        "(u p i) n -> p u (i n)", u=2, i=2
-                    ),
-                )
+        def load_w3(e, g):
+            if g == 0:
+                w3_rows[e] = loads.tile([P, PASSES, PACK, H], BF16, name="w3_rows")
+            nc.sync.dma_start(
+                out=w3_rows[e][:, g].rearrange("p (u i) n -> p u (i n)", i=2),
+                in_=w3[e, g * K_PASS : (g + 1) * K_PASS, :].rearrange(
+                    "(u p i) n -> p u (i n)", u=2, i=2
+                ),
+            )
 
         def load_h2(e):
             h2_rows[e] = loads.tile([P, ROW_TILES, H], BF16, name="h2_rows")
@@ -233,27 +233,17 @@ def tile_ensembledynamicsmodel_pa_t_kernel(
             lo, hi = bounds_of(half)
             r0, count = lo // P, (hi - lo) // P
             if half == 0:
-                mean[e] = work.tile([P, ROW_TILES, O], F32, name="mean")
-                above[e] = work.tile([P, ROW_TILES, O], F32, name="above")
-                offset[e] = work.tile([P, O], F32, name="offset")
-                nc.vector.tensor_tensor(
-                    out=offset[e][:], in0=max_rows[:], in1=b4_rows[:, e, O:O2], op=ALU.subtract
-                )
+                outputs[e] = work.tile([P, ROW_TILES, O2], F32, name="outputs")
             nc.vector.tensor_tensor(
-                out=mean[e][:, r0 : r0 + count, :],
-                in0=acc_out[e, half][:, 0:count, 0:O],
-                in1=b4_rows[:, e, 0:O].unsqueeze(1).to_broadcast([P, count, O]),
+                out=outputs[e][:, r0 : r0 + count, :],
+                in0=acc_out[e, half][:, 0:count, :],
+                in1=shifts[:, e, :].unsqueeze(1).to_broadcast([P, count, O2]),
                 op=ALU.add,
-            )
-            nc.vector.tensor_tensor(
-                out=above[e][:, r0 : r0 + count, :],
-                in0=offset[e][:].unsqueeze(1).to_broadcast([P, count, O]),
-                in1=acc_out[e, half][:, 0:count, O:O2],
-                op=ALU.subtract,
             )
             if half == 1:
                 nc.sync.dma_start(
-                    out=out_0[e].rearrange("(p r) o -> p r o", r=ROW_TILES), in_=mean[e][:]
+                    out=out_0[e].rearrange("(p r) o -> p r o", r=ROW_TILES),
+                    in_=outputs[e][:, :, 0:O],
                 )
 
         def flat(rows):
@@ -267,11 +257,11 @@ def tile_ensembledynamicsmodel_pa_t_kernel(
                 return
             nc.vector.scalar_tensor_tensor(
                 out=clamp[:, e, rows],
-                in0=above[e][:, rows],
+                in0=outputs[e][:, rows, O:O2],
                 scalar=0.0,
                 in1=over(span[:], rows),
-                op0=ALU.max,
-                op1=ALU.subtract,
+                op0=ALU.min,
+                op1=ALU.add,
             )
 
         def bounds_tanh(e, rows=ALL_ROWS):
@@ -281,10 +271,10 @@ def tile_ensembledynamicsmodel_pa_t_kernel(
                 tanh_above[e] = work.tile([P, ROW_TILES, O], F32, name="tanh_above")
                 tanh_w[e] = work.tile([P, ROW_TILES, O], F32, name="tanh_w")
             nc.scalar.activation(
-                out=flat(tanh_above[e][:, rows]), in_=flat(above[e][:, rows]), func=ACT.Abs
+                out=tanh_above[e][:, rows], in_=outputs[e][:, rows, O:O2], func=ACT.Abs
             )
             nc.scalar.activation(
-                out=flat(tanh_w[e][:, rows]), in_=flat(clamp[:, e, rows]), func=ACT.Tanh, scale=-0.5
+                out=flat(tanh_w[e][:, rows]), in_=flat(clamp[:, e, rows]), func=ACT.Tanh, scale=0.5
             )
             nc.scalar.activation(
                 out=flat(tanh_above[e][:, rows]),
@@ -304,8 +294,8 @@ def tile_ensembledynamicsmodel_pa_t_kernel(
                 in0=clamp[:, e, rows],
                 scalar=0.0,
                 in1=over(min_rows[:], rows),
-                op0=ALU.min,
-                op1=ALU.subtract,
+                op0=ALU.max,
+                op1=ALU.add,
             )
 
         def bounds_one_minus(e, rows=ALL_ROWS):
@@ -341,11 +331,23 @@ def tile_ensembledynamicsmodel_pa_t_kernel(
                 bias=half_column[:],
             )
             nc.vector.tensor_tensor(
-                out=clamp[:, e], in0=clamp[:, e], in1=tanh_w_size[:, e], op=ALU.add
+                out=clamp[:, e], in0=clamp[:, e], in1=tanh_w_size[:, e], op=ALU.subtract
             )
 
-        load_w3(0)
+        load_w3(0, 0)
+
+        vectors = consts.tile([P, E * O2 + 2 * O], BF16)
+        nc.vector.memset(vectors[:], 0.0)
+        ones = consts.tile([P, P], BF16)
+        nc.vector.memset(ones[:], 1.0)
+        nc.sync.dma_start(
+            out=vectors[0:1, 0 : E * O2], in_=b4.rearrange("e a o -> (e a o)").unsqueeze(0)
+        )
+        nc.sync.dma_start(out=vectors[0:1, E * O2 : E * O2 + O], in_=max_logvar)
+        nc.sync.dma_start(out=vectors[0:1, E * O2 + O : E * O2 + 2 * O], in_=min_logvar)
+        load_w3(0, 1)
         load_h2(0)
+
         ident_words = consts.tile([P, P], F32)
         make_identity(nc, ident_words[:])
         ident_bf16 = consts.tile([P, P], BF16)
@@ -362,18 +364,9 @@ def tile_ensembledynamicsmodel_pa_t_kernel(
         nc.sync.dma_start(
             out=b3_rows[0 : E * FEATURE_TILES, :], in_=b3.rearrange("e a (m p) -> (e a m) p", p=P)
         )
-        load_w3(1)
+        load_w3(1, 0)
+        load_w3(1, 1)
         load_w4(0)
-
-        vectors = consts.tile([P, E * O2 + 2 * O], BF16)
-        nc.vector.memset(vectors[:], 0.0)
-        ones = consts.tile([P, P], BF16)
-        nc.vector.memset(ones[:], 1.0)
-        nc.sync.dma_start(
-            out=vectors[0:1, 0 : E * O2], in_=b4.rearrange("e a o -> (e a o)").unsqueeze(0)
-        )
-        nc.sync.dma_start(out=vectors[0:1, E * O2 : E * O2 + O], in_=max_logvar)
-        nc.sync.dma_start(out=vectors[0:1, E * O2 + O : E * O2 + 2 * O], in_=min_logvar)
         load_h2(1)
         load_w4(1)
         span = consts.tile([P, O], F32)
@@ -381,7 +374,28 @@ def tile_ensembledynamicsmodel_pa_t_kernel(
         product = consts.tile([P, E, ROW_TILES, O], F32)
         tanh_w_size = consts.tile([P, E, ROW_TILES, O], F32)
 
+        repeated = consts.tile([P, E * O2 + 2 * O], F32)
+        shifts = repeated[:, 0 : E * O2].rearrange("p (e o) -> p e o", e=E)
+        max_rows = repeated[:, E * O2 : E * O2 + O]
+        min_rows = repeated[:, E * O2 + O : E * O2 + 2 * O]
+        sums = {}
+        for c0 in range(0, E * O2 + 2 * O, BANK_COLUMNS):
+            c1 = min(c0 + BANK_COLUMNS, E * O2 + 2 * O)
+            sums[c0] = psum.tile([P, c1 - c0], F32, name="sums", tag="acc_out")
+            nc.tensor.matmul(
+                out=sums[c0][:], lhsT=ones[:], rhs=vectors[:, c0:c1], start=True, stop=True
+            )
         quantise_w3(0)
+        for c0 in range(0, E * O2 + 2 * O, BANK_COLUMNS):
+            c1 = min(c0 + BANK_COLUMNS, E * O2 + 2 * O)
+            nc.vector.tensor_copy(out=repeated[:, c0:c1], in_=sums[c0][:])
+        nc.vector.tensor_tensor(out=span[:], in0=max_rows[:], in1=min_rows[:], op=ALU.subtract)
+        nc.vector.tensor_tensor(
+            out=shifts[:, :, O:O2],
+            in0=shifts[:, :, O:O2],
+            in1=max_rows[:].unsqueeze(1).to_broadcast([P, E, O]),
+            op=ALU.subtract,
+        )
         transpose_h2(0, 0)
         transpose_h2(0, 1)
         b3_flipped = psum.tile([P, P], BF16, name="b3_flipped", tag="bank", bufs=BANKS)
@@ -390,24 +404,11 @@ def tile_ensembledynamicsmodel_pa_t_kernel(
         quantise_h2(0, 1)
         b3_columns = consts.tile([P, E * FEATURE_TILES], F32)
         nc.vector.tensor_copy(out=b3_columns[:], in_=b3_flipped[:, 0 : E * FEATURE_TILES])
-        repeated = consts.tile([P, E * O2 + 2 * O], F32)
-        b4_rows = repeated[:, 0 : E * O2].rearrange("p (e o) -> p e o", e=E)
-        max_rows = repeated[:, E * O2 : E * O2 + O]
-        min_rows = repeated[:, E * O2 + O : E * O2 + 2 * O]
-
-        def repeat_vectors():
-            for c0 in range(0, E * O2 + 2 * O, BANK_COLUMNS):
-                c1 = min(c0 + BANK_COLUMNS, E * O2 + 2 * O)
-                sums = psum.tile([P, c1 - c0], F32, name="sums", tag="bank", bufs=BANKS)
-                nc.tensor.matmul(
-                    out=sums[:], lhsT=ones[:], rhs=vectors[:, c0:c1], start=True, stop=True
-                )
-                nc.vector.tensor_copy(out=repeated[:, c0:c1], in_=sums[:])
-            nc.vector.tensor_tensor(out=span[:], in0=max_rows[:], in1=min_rows[:], op=ALU.subtract)
 
         for e in range(E - 1):
             if e + 2 < E:
-                load_w3(e + 2)
+                load_w3(e + 2, 0)
+                load_w3(e + 2, 1)
                 load_h2(e + 2)
             bounds_minus_w(e - 1)
             quantise_w3(e + 1)
@@ -428,8 +429,6 @@ def tile_ensembledynamicsmodel_pa_t_kernel(
             bounds_one_minus(e - 1)
             quantise_h3(e, 1, 0)
             layer1(e, 1, 1)
-            if e == 0:
-                repeat_vectors()
             transpose_h2(e + 1, 0)
             transpose_h2(e + 1, 1)
             regroup_h3(e, 1, 1)
@@ -492,7 +491,7 @@ def tile_ensembledynamicsmodel_pa_t_kernel(
                     out=product[:, e, rows],
                     in0=product[:, e, rows],
                     in1=clamp[:, e, rows],
-                    op=ALU.subtract,
+                    op=ALU.add,
                 )
                 nc.sync.dma_start(
                     out=out_1[e].rearrange("(p r) o -> p r o", r=ROW_TILES)[:, rows, :],

@@ -39,8 +39,8 @@ def tile_ensembledynamicsmodel_pa_t_kernel(
 
     def interleave(copy, grouped, planes):
         copy(
-            out=grouped.rearrange("p (c i) t -> p c t i", i=4),
-            in_=planes.rearrange("p t (c i) -> p c t i", i=4),
+            out=grouped.rearrange("p (c i) t -> p c t i", i=8),
+            in_=planes.rearrange("p t (c i) -> p c t i", i=8),
         )
 
     with tc.manual_schedule(), tc.tile_pool(name="consts", bufs=1) as consts, tc.tile_pool(

import concourse.mybir as mybir
from concourse.masks import make_identity

F32 = mybir.dt.float32
BF16 = mybir.dt.bfloat16
U32 = mybir.dt.uint32
U8 = mybir.dt.uint8
FP8X4 = mybir.dt.float8_e4m3fn_x4
ACT = mybir.ActivationFunctionType
ALU = mybir.AluOpType

P = 128
PACK = 4
K_PASS = P * PACK
E, B, H, O = 5, 896, 1024, 64
O2 = 2 * O
PASSES = H // K_PASS
ROW_TILES = B // P
FEATURE_TILES = H // P
W3_CHUNK = 512
SCALAR_COLUMNS = (512, 384)
COLUMN_HALVES = (((0, 512),), ((512, 768), (768, 896)))
BANK_COLUMNS = 512
BANKS = 6
ALL_ROWS = slice(0, ROW_TILES)
HALF_ROWS = (slice(0, 4), slice(4, ROW_TILES))

FLOPS = 2 * E * B * H * (H + O2)


def tile_ensembledynamicsmodel_pa_t_kernel(
    tc, h2, w3, b3, w4, b4, max_logvar, min_logvar, out_0, out_1
):
    nc = tc.nc

    def bounds_of(half):
        chunks = COLUMN_HALVES[half]
        return chunks[0][0], chunks[-1][1]

    def interleave(copy, grouped, planes):
        copy(
            out=grouped.rearrange("p (c i) t -> p c t i", i=8),
            in_=planes.rearrange("p t (c i) -> p c t i", i=8),
        )

    with tc.manual_schedule(), tc.tile_pool(name="consts", bufs=1) as consts, tc.tile_pool(
        name="loads", bufs=2
    ) as loads, tc.tile_pool(name="work", bufs=2) as work, tc.tile_pool(
        name="codes", bufs=2
    ) as codes, tc.psum_pool(name="psum", bufs=2) as psum:
        w3_rows, h2_rows, w4_rows, w4_grouped = {}, {}, {}, {}
        w3_codes, w3_scales, h2_grouped, h2_codes, h2_scales = {}, {}, {}, {}, {}
        h3_planes, h3_grouped, h3_codes, h3_scales, w4_codes, w4_scales = {}, {}, {}, {}, {}, {}
        acc_out, outputs, tanh_above, tanh_w = {}, {}, {}, {}

        def load_w3(e, g):
            if g == 0:
                w3_rows[e] = loads.tile([P, PASSES, PACK, H], BF16, name="w3_rows")
            nc.sync.dma_start(
                out=w3_rows[e][:, g].rearrange("p (u i) n -> p u (i n)", i=2),
                in_=w3[e, g * K_PASS : (g + 1) * K_PASS, :].rearrange(
                    "(u p i) n -> p u (i n)", u=2, i=2
                ),
            )

        def load_h2(e):
            h2_rows[e] = loads.tile([P, ROW_TILES, H], BF16, name="h2_rows")
            for half in range(2):
                lo, hi = bounds_of(half)
                nc.sync.dma_start(
                    out=h2_rows[e][:, lo // P : hi // P, :],
                    in_=h2[e].rearrange("(p r) k -> p r k", r=ROW_TILES)[:, lo // P : hi // P, :],
                )

        def load_w4(e):
            w4_rows[e] = loads.tile([P, PASSES * PACK, O2], BF16, name="w4_rows")
            nc.sync.dma_start(out=w4_rows[e][:], in_=w4[e].rearrange("(j p) o -> p j o", p=P))

        def quantise_w3(e):
            if e >= E:
                return
            w3_codes[e] = codes.tile([P, PASSES, H], U32, name="w3_codes", align_bytes=64)
            w3_scales[e] = codes.tile([P, PASSES, H], U8, name="w3_scales", align_bytes=64)
            grouped = {}
            for n0 in range(0, H, W3_CHUNK):
                for g in range(PASSES):
                    w3_grouped = work.tile(
                        [P, W3_CHUNK, PACK], BF16, name="w3_grouped", bufs=4, align_bytes=64
                    )
                    grouped[n0, g] = w3_grouped
                    mine = W3_CHUNK if n0 == 0 else W3_CHUNK - SCALAR_COLUMNS[g]
                    if mine > 0:
                        interleave(
                            nc.vector.tensor_copy,
                            w3_grouped[:, 0:mine, :],
                            w3_rows[e][:, g, :, n0 : n0 + mine],
                        )
                    if mine < W3_CHUNK:
                        interleave(
                            nc.scalar.copy,
                            w3_grouped[:, mine:W3_CHUNK, :],
                            w3_rows[e][:, g, :, n0 + mine : n0 + W3_CHUNK],
                        )
            for n0 in range(0, H, W3_CHUNK):
                for g in range(PASSES):
                    nc.vector.quantize_mx(
                        out=w3_codes[e][:, g, n0 : n0 + W3_CHUNK].bitcast(FP8X4),
                        scales=w3_scales[e][:, g, n0 : n0 + W3_CHUNK],
                        in_=grouped[n0, g][:].rearrange("p n t -> p (n t)"),
                    )

        def regroup_w4(e):
            if e >= E:
                return
            w4_grouped[e] = work.tile(
                [P, PASSES, O2, PACK], BF16, name="w4_grouped", bufs=1, align_bytes=64
            )
            nc.vector.tensor_copy(
                out=w4_grouped[e][:], in_=w4_rows[e][:].rearrange("p (g t) o -> p g o t", t=PACK)
            )

        def quantise_w4(e):
            if e >= E:
                return
            w4_codes[e] = codes.tile([P, PASSES, O2], U32, name="w4_codes", align_bytes=64)
            w4_scales[e] = codes.tile([P, PASSES, O2], U8, name="w4_scales", align_bytes=64)
            nc.vector.quantize_mx(
                out=w4_codes[e][:].rearrange("p g o -> p (g o)").bitcast(FP8X4),
                scales=w4_scales[e][:].rearrange("p g o -> p (g o)"),
                in_=w4_grouped[e][:].rearrange("p g o t -> p (g o t)"),
            )

        def transpose_h2(e, half):
            if e >= E:
                return
            if half == 0:
                h2_grouped[e] = work.tile(
                    [P, PASSES * B * PACK], BF16, name="h2_grouped", bufs=1, align_bytes=64
                )
            words_in = h2_rows[e][:].rearrange("p r k -> p (r k)").bitcast(F32)
            words_out = h2_grouped[e][:].bitcast(F32).rearrange(
                "p (g c u) -> p g c u", g=PASSES, u=2
            )
            blocks = H // 2 // P
            lo, hi = bounds_of(half)
            for r in range(lo // P, hi // P):
                flipped = psum.tile([P, blocks, P], F32, name="flipped", tag="bank", bufs=BANKS)
                for j in range(blocks):
                    w0 = (r * blocks + j) * P
                    nc.tensor.transpose(flipped[:, j, :], words_in[:, w0 : w0 + P], ident_words[:])
                nc.scalar.copy(
                    out=words_out[:, :, r * P : (r + 1) * P, :],
                    in_=flipped[:].rearrange("p (g u) c -> p g c u", u=2),
                )

        def quantise_h2(e, half):
            if e >= E:
                return
            if half == 0:
                h2_codes[e] = codes.tile([P, PASSES, B], U32, name="h2_codes", align_bytes=64)
                h2_scales[e] = codes.tile([P, PASSES, B], U8, name="h2_scales", align_bytes=64)
            for c0, c1 in COLUMN_HALVES[half]:
                for g in range(PASSES):
                    nc.vector.quantize_mx(
                        out=h2_codes[e][:, g, c0:c1].bitcast(FP8X4),
                        scales=h2_scales[e][:, g, c0:c1],
                        in_=h2_grouped[e][:, (g * B + c0) * PACK : (g * B + c1) * PACK],
                    )

        def layer1(e, half, g_out):
            lo, hi = bounds_of(half)
            planes = work.tile([P, PACK, hi - lo], BF16, name="h3_planes%d" % half)
            h3_planes[e, half, g_out] = planes
            for t in range(PACK):
                m = g_out * PACK + t
                acc = psum.tile([P, hi - lo], F32, name="acc", tag="bank", bufs=BANKS)
                for c0, c1 in COLUMN_HALVES[half]:
                    for g in range(PASSES):
                        nc.tensor.matmul_mx(
                            out=acc[:, c0 - lo : c1 - lo],
                            lhsT=w3_codes[e][:, g, m * P : (m + 1) * P].bitcast(FP8X4),
                            lhsT_scale=w3_scales[e][:, g, m * P : (m + 1) * P],
                            rhs=h2_codes[e][:, g, c0:c1].bitcast(FP8X4),
                            rhs_scale=h2_scales[e][:, g, c0:c1],
                            start=(g == 0),
                            stop=(g == PASSES - 1),
                        )
                nc.scalar.activation(
                    out=planes[:, t, :],
                    in_=acc[:],
                    func=ACT.Silu,
                    bias=b3_columns[:, e * FEATURE_TILES + m : e * FEATURE_TILES + m + 1],
                )

        def regroup_h3(e, half, g_out):
            lo, hi = bounds_of(half)
            grouped = work.tile(
                [P, hi - lo, PACK], BF16, name="h3_grouped%d" % half, align_bytes=64
            )
            h3_grouped[e, half, g_out] = grouped
            interleave(nc.vector.tensor_copy, grouped[:], h3_planes[e, half, g_out][:])

        def quantise_h3(e, half, g_out):
            if half == 0 and g_out == 0:
                h3_codes[e] = codes.tile([P, PASSES, B], U32, name="h3_codes", align_bytes=64)
                h3_scales[e] = codes.tile([P, PASSES, B], U8, name="h3_scales", align_bytes=64)
            lo, hi = bounds_of(half)
            for c0, c1 in COLUMN_HALVES[half]:
                nc.vector.quantize_mx(
                    out=h3_codes[e][:, g_out, c0:c1].bitcast(FP8X4),
                    scales=h3_scales[e][:, g_out, c0:c1],
                    in_=h3_grouped[e, half, g_out][:, c0 - lo : c1 - lo, :].rearrange(
                        "p c t -> p (c t)"
                    ),
                )

        def layer2_products(e, half):
            lo, hi = bounds_of(half)
            acc_out[e, half] = psum.tile([P, BANK_COLUMNS // O2, O2], F32, name="acc_out")
            for r in range(lo // P, hi // P):
                for g in range(PASSES):
                    nc.tensor.matmul_mx(
                        out=acc_out[e, half][:, r - lo // P, :],
                        lhsT=h3_codes[e][:, g, r * P : (r + 1) * P].bitcast(FP8X4),
                        lhsT_scale=h3_scales[e][:, g, r * P : (r + 1) * P],
                        rhs=w4_codes[e][:, g, :].bitcast(FP8X4),
                        rhs_scale=w4_scales[e][:, g, :],
                        start=(g == 0),
                        stop=(g == PASSES - 1),
                    )

        def layer2_outputs(e, half):
            lo, hi = bounds_of(half)
            r0, count = lo // P, (hi - lo) // P
            if half == 0:
                outputs[e] = work.tile([P, ROW_TILES, O2], F32, name="outputs")
            nc.vector.tensor_tensor(
                out=outputs[e][:, r0 : r0 + count, :],
                in0=acc_out[e, half][:, 0:count, :],
                in1=shifts[:, e, :].unsqueeze(1).to_broadcast([P, count, O2]),
                op=ALU.add,
            )
            if half == 1:
                nc.sync.dma_start(
                    out=out_0[e].rearrange("(p r) o -> p r o", r=ROW_TILES),
                    in_=outputs[e][:, :, 0:O],
                )

        def flat(rows):
            return rows.rearrange("p r o -> p (r o)")

        def over(row, rows):
            return row.unsqueeze(1).to_broadcast([P, rows.stop - rows.start, O])

        def bounds_minus_w(e, rows=ALL_ROWS):
            if e < 0:
                return
            nc.vector.scalar_tensor_tensor(
                out=clamp[:, e, rows],
                in0=outputs[e][:, rows, O:O2],
                scalar=0.0,
                in1=over(span[:], rows),
                op0=ALU.min,
                op1=ALU.add,
            )

        def bounds_tanh(e, rows=ALL_ROWS):
            if e < 0:
                return
            if rows.start == 0:
                tanh_above[e] = work.tile([P, ROW_TILES, O], F32, name="tanh_above")
                tanh_w[e] = work.tile([P, ROW_TILES, O], F32, name="tanh_w")
            nc.scalar.activation(
                out=tanh_above[e][:, rows], in_=outputs[e][:, rows, O:O2], func=ACT.Abs
            )
            nc.scalar.activation(
                out=flat(tanh_w[e][:, rows]), in_=flat(clamp[:, e, rows]), func=ACT.Tanh, scale=0.5
            )
            nc.scalar.activation(
                out=flat(tanh_above[e][:, rows]),
                in_=flat(tanh_above[e][:, rows]),
                func=ACT.Tanh,
                scale=0.5,
            )
            nc.scalar.activation(
                out=flat(tanh_w_size[:, e, rows]), in_=flat(tanh_w[e][:, rows]), func=ACT.Abs
            )

        def bounds_clamp(e, rows=ALL_ROWS):
            if e < 0:
                return
            nc.vector.scalar_tensor_tensor(
                out=clamp[:, e, rows],
                in0=clamp[:, e, rows],
                scalar=0.0,
                in1=over(min_rows[:], rows),
                op0=ALU.max,
                op1=ALU.add,
            )

        def bounds_one_minus(e, rows=ALL_ROWS):
            if e < 0:
                return
            nc.vector.tensor_scalar(
                out=tanh_above[e][:, rows],
                in0=tanh_above[e][:, rows],
                scalar1=-1.0,
                scalar2=1.0,
                op0=ALU.mult,
                op1=ALU.add,
            )

        def bounds_product(e, rows=ALL_ROWS):
            if e < 0:
                return
            nc.vector.scalar_tensor_tensor(
                out=product[:, e, rows],
                in0=tanh_w[e][:, rows],
                scalar=1.0,
                in1=tanh_above[e][:, rows],
                op0=ALU.add,
                op1=ALU.mult,
            )

        def logarithm_of_size(e):
            nc.scalar.activation(
                out=flat(tanh_w_size[:, e]),
                in_=flat(tanh_w_size[:, e]),
                func=ACT.Ln,
                scale=0.5,
                bias=half_column[:],
            )
            nc.vector.tensor_tensor(
                out=clamp[:, e], in0=clamp[:, e], in1=tanh_w_size[:, e], op=ALU.subtract
            )

        load_w3(0, 0)

        vectors = consts.tile([P, E * O2 + 2 * O], BF16)
        nc.vector.memset(vectors[:], 0.0)
        ones = consts.tile([P, P], BF16)
        nc.vector.memset(ones[:], 1.0)
        nc.sync.dma_start(
            out=vectors[0:1, 0 : E * O2], in_=b4.rearrange("e a o -> (e a o)").unsqueeze(0)
        )
        nc.sync.dma_start(out=vectors[0:1, E * O2 : E * O2 + O], in_=max_logvar)
        nc.sync.dma_start(out=vectors[0:1, E * O2 + O : E * O2 + 2 * O], in_=min_logvar)
        load_w3(0, 1)
        load_h2(0)

        ident_words = consts.tile([P, P], F32)
        make_identity(nc, ident_words[:])
        ident_bf16 = consts.tile([P, P], BF16)
        make_identity(nc, ident_bf16[:])
        half_column = consts.tile([P, 1], F32)
        nc.vector.memset(half_column[:], 0.5)
        one_column = consts.tile([P, 1], F32)
        nc.vector.memset(one_column[:], 1.0)
        table_warmer = consts.tile([P, 1], F32)
        nc.scalar.activation(out=table_warmer[:], in_=one_column[:], func=ACT.Silu)

        b3_rows = consts.tile([P, P], BF16)
        nc.vector.memset(b3_rows[:], 0.0)
        nc.sync.dma_start(
            out=b3_rows[0 : E * FEATURE_TILES, :], in_=b3.rearrange("e a (m p) -> (e a m) p", p=P)
        )
        load_w3(1, 0)
        load_w3(1, 1)
        load_w4(0)
        load_h2(1)
        load_w4(1)
        span = consts.tile([P, O], F32)
        clamp = consts.tile([P, E, ROW_TILES, O], F32)
        product = consts.tile([P, E, ROW_TILES, O], F32)
        tanh_w_size = consts.tile([P, E, ROW_TILES, O], F32)

        repeated = consts.tile([P, E * O2 + 2 * O], F32)
        shifts = repeated[:, 0 : E * O2].rearrange("p (e o) -> p e o", e=E)
        max_rows = repeated[:, E * O2 : E * O2 + O]
        min_rows = repeated[:, E * O2 + O : E * O2 + 2 * O]
        sums = {}
        for c0 in range(0, E * O2 + 2 * O, BANK_COLUMNS):
            c1 = min(c0 + BANK_COLUMNS, E * O2 + 2 * O)
            sums[c0] = psum.tile([P, c1 - c0], F32, name="sums", tag="acc_out")
            nc.tensor.matmul(
                out=sums[c0][:], lhsT=ones[:], rhs=vectors[:, c0:c1], start=True, stop=True
            )
        quantise_w3(0)
        for c0 in range(0, E * O2 + 2 * O, BANK_COLUMNS):
            c1 = min(c0 + BANK_COLUMNS, E * O2 + 2 * O)
            nc.vector.tensor_copy(out=repeated[:, c0:c1], in_=sums[c0][:])
        nc.vector.tensor_tensor(out=span[:], in0=max_rows[:], in1=min_rows[:], op=ALU.subtract)
        nc.vector.tensor_tensor(
            out=shifts[:, :, O:O2],
            in0=shifts[:, :, O:O2],
            in1=max_rows[:].unsqueeze(1).to_broadcast([P, E, O]),
            op=ALU.subtract,
        )
        transpose_h2(0, 0)
        transpose_h2(0, 1)
        b3_flipped = psum.tile([P, P], BF16, name="b3_flipped", tag="bank", bufs=BANKS)
        nc.tensor.transpose(b3_flipped[:], b3_rows[:], ident_bf16[:])
        quantise_h2(0, 0)
        quantise_h2(0, 1)
        b3_columns = consts.tile([P, E * FEATURE_TILES], F32)
        nc.vector.tensor_copy(out=b3_columns[:], in_=b3_flipped[:, 0 : E * FEATURE_TILES])

        for e in range(E - 1):
            if e + 2 < E:
                load_w3(e + 2, 0)
                load_w3(e + 2, 1)
                load_h2(e + 2)
            bounds_minus_w(e - 1)
            quantise_w3(e + 1)
            layer1(e, 0, 0)
            regroup_h3(e, 0, 0)
            regroup_w4(e)
            quantise_h3(e, 0, 0)
            if e + 2 < E:
                load_w4(e + 2)
            layer1(e, 0, 1)
            bounds_tanh(e - 1)
            regroup_h3(e, 0, 1)
            quantise_w4(e)
            quantise_h3(e, 0, 1)
            layer1(e, 1, 0)
            regroup_h3(e, 1, 0)
            bounds_clamp(e - 1)
            bounds_one_minus(e - 1)
            quantise_h3(e, 1, 0)
            layer1(e, 1, 1)
            transpose_h2(e + 1, 0)
            transpose_h2(e + 1, 1)
            regroup_h3(e, 1, 1)
            bounds_product(e - 1)
            quantise_h3(e, 1, 1)
            quantise_h2(e + 1, 0)
            layer2_products(e, 0)
            layer2_outputs(e, 0)
            quantise_h2(e + 1, 1)
            layer2_products(e, 1)
            layer2_outputs(e, 1)

        e = E - 1
        layer1(e, 0, 0)
        regroup_h3(e, 0, 0)
        bounds_minus_w(e - 1)
        regroup_w4(e)
        quantise_h3(e, 0, 0)
        layer1(e, 0, 1)
        regroup_h3(e, 0, 1)
        quantise_w4(e)
        quantise_h3(e, 0, 1)
        layer1(e, 1, 0)
        layer1(e, 1, 1)
        layer2_products(e, 0)
        regroup_h3(e, 1, 0)
        layer2_outputs(e, 0)
        quantise_h3(e, 1, 0)
        regroup_h3(e, 1, 1)
        bounds_minus_w(e, HALF_ROWS[0])
        quantise_h3(e, 1, 1)
        bounds_tanh(e - 1)
        bounds_tanh(e, HALF_ROWS[0])
        layer2_products(e, 1)
        layer2_outputs(e, 1)
        bounds_minus_w(e, HALF_ROWS[1])
        bounds_tanh(e, HALF_ROWS[1])
        bounds_clamp(e - 1)
        bounds_one_minus(e - 1)
        bounds_clamp(e, HALF_ROWS[0])
        bounds_product(e - 1)
        bounds_one_minus(e, HALF_ROWS[0])
        bounds_clamp(e, HALF_ROWS[1])
        bounds_product(e, HALF_ROWS[0])
        bounds_one_minus(e, HALF_ROWS[1])
        logarithm_of_size(0)
        bounds_product(e, HALF_ROWS[1])
        for e in range(E):
            if e > 0:
                logarithm_of_size(e)
            for rows in HALF_ROWS if e == E - 1 else (ALL_ROWS,):
                nc.scalar.activation(
                    out=flat(product[:, e, rows]),
                    in_=flat(product[:, e, rows]),
                    func=ACT.Ln,
                    scale=-0.25,
                    bias=one_column[:],
                )
                nc.vector.tensor_tensor(
                    out=product[:, e, rows],
                    in0=product[:, e, rows],
                    in1=clamp[:, e, rows],
                    op=ALU.add,
                )
                nc.sync.dma_start(
                    out=out_1[e].rearrange("(p r) o -> p r o", r=ROW_TILES)[:, rows, :],
                    in_=product[:, e, rows],
                )
